import numpy as np
import ml_dtypes


def mxq(x, axis, fmt="e4m3"):
    dtype, down = {"e4m3": (ml_dtypes.float8_e4m3fn, 7), "e5m2": (ml_dtypes.float8_e5m2, 14)}[fmt]
    v = np.moveaxis(np.asarray(x, np.float32).astype(ml_dtypes.bfloat16).astype(np.float64), axis, -1)
    blocks = v.reshape(v.shape[:-1] + (-1, 32))
    amax = np.abs(blocks).max(-1, keepdims=True)
    byte = np.maximum(np.where(amax > 0, np.frexp(amax)[1] - 1 + 127, 0) - down, 1)
    scale = np.exp2(byte - 127.0)
    codes = (blocks / scale).astype(np.float32).astype(dtype).astype(np.float64)
    return np.moveaxis((codes * scale).reshape(v.shape), -1, axis)


WIDE = False


def mx_kscale(k):
    if not WIDE:
        return np.ones(k)
    levels = np.array([10, -10, 5, -5, 0])
    a = np.random.permutation(np.resize(levels, k // 512 * 4)).reshape(k // 512, 4)
    idx = np.arange(k)
    return np.exp2(a[idx // 512, idx % 128 // 32])


BF16 = ml_dtypes.bfloat16


def bf(x):
    return np.asarray(x, np.float32).astype(BF16)


def f64(x):
    return np.asarray(x).astype(np.float64)


B, MID, H1, H2, C, E, OD = 64, 128, 64, 32, 16, 2048, 16
OS = 0.5 * np.sqrt(C)
LAM = 1.3 / (C * E) ** 0.25


def softmax(v):
    e = np.exp(v - v.max(-1, keepdims=True))
    return e / e.sum(-1, keepdims=True)


def setup_inputs():
    s, t = mx_kscale(E), mx_kscale(E)
    f = np.concatenate([np.tile(s, (C, 1)), np.tile(1.0 / t, (C, 1))], 0)
    return {
        "h_towers": bf(np.maximum(np.random.standard_normal((B, 2 * C)) * OS, 0.0)),
        "W_emb": bf(np.random.standard_normal((2 * C, E)) * 1.2 * LAM / OS * f),
        "b_emb": bf(np.random.standard_normal((2 * C, E)) * 0.5 * LAM * f),
        "M": bf(np.random.standard_normal((E, E)) / np.sqrt(E) * t[None, :] / s[:, None]),
    }


def reference(h_towers, W_emb, b_emb, M):
    h = f64(h_towers)
    emb = h[:, :, None] * f64(W_emb)[None, :, :] + f64(b_emb)[None, :, :]
    l, r = emb[:, :C, :], emb[:, C:, :]
    u = mxq(l, 2, "e4m3") @ mxq(f64(M), 0, "e4m3")
    G = np.tanh(mxq(u, 2, "e4m3") @ mxq(r, 2, "e4m3").transpose(0, 2, 1))
    lr = softmax(G.sum(axis=1))
    rl = softmax(G.sum(axis=2))
    a = np.concatenate([lr, rl], axis=-1)
    return h * a

@@ -1,0 +1,304 @@
+from contextlib import ExitStack
+
+import concourse.mybir as mybir
+from concourse.masks import make_identity
+
+F32 = mybir.dt.float32
+BF16 = mybir.dt.bfloat16
+U32 = mybir.dt.uint32
+U8 = mybir.dt.uint8
+FP8X4 = mybir.dt.float8_e4m3fn_x4
+ACT = mybir.ActivationFunctionType
+ALU = mybir.AluOpType
+AX = mybir.AxisListType
+
+P = 128
+PACK = 4
+K_PASS = P * PACK
+B = 64
+C = 16
+E = 2048
+PASSES = E // K_PASS
+SLOTS = E // P
+TILE_B = P // C
+ROW_TILES = B // TILE_B
+ROWS = B * C
+CHUNK = K_PASS
+R_UNITS_PER_BANK = 3
+
+FLOPS = 2 * ROWS * E * E + 2 * B * C * C * E
+
+
+def tile_mlp_embedding_layer_pa_kernel(tc, h_towers, W_emb, b_emb, M, out):
+    nc = tc.nc
+    with ExitStack() as ctx:
+        const = ctx.enter_context(tc.tile_pool(name="const", bufs=1))
+        keep = ctx.enter_context(tc.tile_pool(name="keep", bufs=1))
+        m_in = ctx.enter_context(tc.tile_pool(name="m_in", bufs=2))
+        m_words = ctx.enter_context(tc.tile_pool(name="m_words", bufs=3))
+        wide = ctx.enter_context(tc.tile_pool(name="wide", bufs=4))
+        work = ctx.enter_context(tc.tile_pool(name="work", bufs=4))
+        small = ctx.enter_context(tc.tile_pool(name="small", bufs=1))
+        psum = ctx.enter_context(tc.psum_pool(name="psum", bufs=8))
+
+        def load_m(chunk):
+            m_raw = m_in.tile([P, SLOTS, CHUNK], BF16)
+            nc.sync.dma_start(
+                out=m_raw[:],
+                in_=M.rearrange("(a p) n -> p a n", p=P)[:, :, chunk * CHUNK : (chunk + 1) * CHUNK],
+            )
+            return m_raw
+
+        m_raw_of = {0: load_m(0)}
+
+        h_all = const.tile([P, B, 2 * C], BF16)
+        nc.scalar.dma_start(
+            out=h_all[:].rearrange("p b c -> p (b c)"),
+            in_=h_towers.rearrange("b c -> (b c)").partition_broadcast(P),
+        )
+
+        emb_l = const.tile([P, PASSES, P], BF16)
+        for w, table in enumerate((W_emb, b_emb)):
+            runs = table[0:C, :].rearrange("c (g t p) -> t c g p", t=PACK, p=P)
+            for t in range(PACK):
+                first = 64 * w + C * t
+                nc.scalar.dma_start(out=emb_l[first : first + C, :, :], in_=runs[t])
+
+        m_raw_of[1] = load_m(1)
+
+        emb_rows = const.tile([P, E], BF16)
+        nc.sync.dma_start(out=emb_rows[0 : 2 * C, :], in_=W_emb)
+        nc.sync.dma_start(out=emb_rows[2 * C : 4 * C, :], in_=b_emb)
+
+        h_out = small.tile([2 * ROW_TILES, TILE_B, C], BF16)
+        for s in range(2):
+            nc.sync.dma_start(
+                out=h_out[s * ROW_TILES : (s + 1) * ROW_TILES, :, :],
+                in_=h_towers[:, s * C : (s + 1) * C].rearrange("(r l) c -> r l c", l=TILE_B),
+            )
+
+        ident_bf = const.tile([P, P], BF16)
+        make_identity(nc, ident_bf[:])
+        ident_f32 = const.tile([P, P], F32)
+        make_identity(nc, ident_f32[:])
+
+        pick = const.tile([P, C, PACK], BF16)
+        nc.vector.tensor_tensor(
+            out=pick[:],
+            in0=ident_bf[:, 0:64].rearrange("p (t c) -> p c t", t=PACK),
+            in1=ident_bf[:, 64:128].rearrange("p (t c) -> p c t", t=PACK),
+            op=ALU.add,
+        )
+
+        same_l = const.tile([P, TILE_B], F32)
+        nc.vector.tensor_reduce(
+            out=same_l[:], in_=ident_f32[:].rearrange("p (c l) -> p l c", l=TILE_B), axis=AX.X, op=ALU.add
+        )
+        same_batch = const.tile([P, C, TILE_B], F32)
+        nc.vector.tensor_copy(out=same_batch[:], in_=same_l[:].unsqueeze(1).to_broadcast([P, C, TILE_B]))
+
+        sums = small.tile([P, P], F32)
+        nc.gpsimd.memset(sums[:], 0.0)
+        nc.gpsimd.memset(emb_rows[64:128, :], 0.0)
+
+        m_codes = keep.tile([P, PASSES, E], U32, align_bytes=64)
+        m_scales = keep.tile([P, PASSES, E], U8, align_bytes=64)
+        l_codes = keep.tile([P, ROW_TILES // 2, PASSES, 2 * P], U32, align_bytes=64)
+        l_scales = keep.tile([P, ROW_TILES // 2, PASSES, 2 * P], U8, align_bytes=64)
+        u_codes = keep.tile([P, PASSES, ROWS], U32, align_bytes=64)
+        u_scales = keep.tile([P, PASSES, ROWS], U8, align_bytes=64)
+        r_codes = keep.tile([P, PASSES, ROWS], U32, align_bytes=64)
+        r_scales = keep.tile([P, PASSES, ROWS], U8, align_bytes=64)
+
+        spread = const.tile([P, ROW_TILES, C, TILE_B, PACK], BF16)
+        for rt in range(ROW_TILES):
+            nc.vector.tensor_copy(
+                out=spread[64:128, rt],
+                in_=pick[64:128].unsqueeze(2).to_broadcast([64, C, TILE_B, PACK]),
+            )
+
+        def make_l(pair):
+            for rt in (2 * pair, 2 * pair + 1):
+                nc.vector.tensor_tensor(
+                    out=spread[0:64, rt],
+                    in0=h_all[0:64, rt * TILE_B : (rt + 1) * TILE_B, 0:C]
+                    .rearrange("p l c -> p c l")
+                    .unsqueeze(3)
+                    .to_broadcast([64, C, TILE_B, PACK]),
+                    in1=pick[0:64].unsqueeze(2).to_broadcast([64, C, TILE_B, PACK]),
+                    op=ALU.mult,
+                )
+            l_bf = wide.tile([P, PASSES, 2 * K_PASS], BF16, tag="wide", align_bytes=64)
+            for g in range(PASSES):
+                l_bank = psum.tile([P, 2, K_PASS], BF16, tag="bank")
+                for half in range(2):
+                    nc.tensor.matmul(
+                        out=l_bank[:, half, :],
+                        lhsT=emb_l[:, g, :],
+                        rhs=spread[:, 2 * pair + half].rearrange("p c l t -> p (c l t)"),
+                        start=True,
+                        stop=True,
+                    )
+                nc.scalar.copy(out=l_bf[:, g, :], in_=l_bank[:].rearrange("p h w -> p (h w)"))
+            nc.vector.quantize_mx(
+                out=l_codes[:, pair].rearrange("p g w -> p (g w)").bitcast(FP8X4),
+                scales=l_scales[:, pair].rearrange("p g w -> p (g w)"),
+                in_=l_bf[:].rearrange("p g w -> p (g w)"),
+            )
+
+        def quantise_m(chunk):
+            m_raw = m_raw_of[chunk]
+            cols = slice(chunk * CHUNK, (chunk + 1) * CHUNK)
+            for g in range(PASSES):
+                m_bf = m_words.tile([P, CHUNK, PACK], BF16, align_bytes=64)
+                nc.vector.tensor_copy(
+                    out=m_bf[:].rearrange("p (c i) t -> p c t i", i=4),
+                    in_=m_raw[:, g * PACK : (g + 1) * PACK, :].rearrange("p t (c i) -> p c t i", i=4),
+                )
+                nc.vector.quantize_mx(
+                    out=m_codes[:, g, cols].bitcast(FP8X4),
+                    scales=m_scales[:, g, cols],
+                    in_=m_bf[:].rearrange("p n t -> p (n t)"),
+                )
+
+        emb_t = const.tile([P, SLOTS, 4 * C], F32)
+        h_right = const.tile([P, C, B], BF16)
+
+        def prepare_r():
+            for half in range(2):
+                t_bank = psum.tile([P, SLOTS // 2, P], BF16, tag="bank")
+                for i in range(SLOTS // 2):
+                    a = half * (SLOTS // 2) + i
+                    nc.tensor.transpose(out=t_bank[:, i, :], in_=emb_rows[:, a * P : (a + 1) * P], identity=ident_bf[:])
+                nc.vector.tensor_copy(
+                    out=emb_t[:, half * (SLOTS // 2) : (half + 1) * (SLOTS // 2), :], in_=t_bank[:, :, 0 : 4 * C]
+                )
+            nc.gpsimd.tensor_copy(out=h_right[:], in_=h_all[:, :, C : 2 * C].rearrange("p b c -> p c b"))
+
+        r_parts_of = {}
+
+        def make_r_unit(g, j):
+            if j == 0:
+                r_parts_of[g] = wide.tile([P, ROW_TILES, C, PACK, TILE_B], BF16, tag="wide", name="r_parts", align_bytes=64)
+            for t in range(PACK):
+                a = g * PACK + t
+                nc.scalar.activation(
+                    out=r_parts_of[g][:, :, j, t, :],
+                    in_=h_right[:, j, :].rearrange("p (r l) -> p r l", l=TILE_B),
+                    func=ACT.Identity,
+                    scale=emb_t[:, a, C + j : C + j + 1],
+                    bias=emb_t[:, a, 3 * C + j : 3 * C + j + 1],
+                )
+            if j == C - 1:
+                r_bf = wide.tile([P, ROW_TILES * C, TILE_B, PACK], BF16, tag="wide", align_bytes=64)
+                nc.vector.tensor_copy(out=r_bf[:], in_=r_parts_of[g][:].rearrange("p r j t l -> p (r j) l t"))
+                nc.vector.quantize_mx(
+                    out=r_codes[:, g, :].bitcast(FP8X4),
+                    scales=r_scales[:, g, :],
+                    in_=r_bf[:].rearrange("p a l t -> p (a l t)"),
+                )
+
+        def make_u(g2, rt):
+            rows = slice(rt * P, (rt + 1) * P)
+            l_rows = slice((rt % 2) * P, (rt % 2 + 1) * P)
+            u_bank = psum.tile([P, PACK, P], F32, tag="bank")
+            for t in range(PACK):
+                n_cols = slice((g2 * PACK + t) * P, (g2 * PACK + t + 1) * P)
+                for g in range(PASSES):
+                    nc.tensor.matmul_mx(
+                        out=u_bank[:, t, :],
+                        lhsT=m_codes[:, g, n_cols].bitcast(FP8X4),
+                        lhsT_scale=m_scales[:, g, n_cols],
+                        rhs=l_codes[:, rt // 2, g, l_rows].bitcast(FP8X4),
+                        rhs_scale=l_scales[:, rt // 2, g, l_rows],
+                        start=(g == 0),
+                        stop=(g == PASSES - 1),
+                    )
+            u_bf = work.tile([P, P, PACK], BF16, align_bytes=64)
+            nc.scalar.copy(out=u_bf[:], in_=u_bank[:].rearrange("p t r -> p r t"))
+            nc.vector.quantize_mx(
+                out=u_codes[:, g2, rows].bitcast(FP8X4),
+                scales=u_scales[:, g2, rows],
+                in_=u_bf[:].rearrange("p r t -> p (r t)"),
+            )
+
+        def make_sums(pair):
+            g_bank = psum.tile([P, 4, P], F32, tag="bank")
+            for half in range(2):
+                rows = slice((2 * pair + half) * P, (2 * pair + half + 1) * P)
+                for s in range(2):
+                    on_part = (r_codes, r_scales) if s == 0 else (u_codes, u_scales)
+                    on_free = (u_codes, u_scales) if s == 0 else (r_codes, r_scales)
+                    for g in range(PASSES):
+                        nc.tensor.matmul_mx(
+                            out=g_bank[:, 2 * half + s, :],
+                            lhsT=on_part[0][:, g, rows].bitcast(FP8X4),
+                            lhsT_scale=on_part[1][:, g, rows],
+                            rhs=on_free[0][:, g, rows].bitcast(FP8X4),
+                            rhs_scale=on_free[1][:, g, rows],
+                            start=(g == 0),
+                            stop=(g == PASSES - 1),
+                        )
+            own = work.tile([P, 4, P], F32)
+            nc.vector.tensor_tensor(
+                out=own[:],
+                in0=g_bank[:],
+                in1=same_batch[:].rearrange("p c l -> p (c l)").unsqueeze(1).to_broadcast([P, 4, P]),
+                op=ALU.mult,
+            )
+            for half in range(2):
+                for s in range(2):
+                    column = s * ROW_TILES + 2 * pair + half
+                    tanh_g = work.tile([P, P], F32)
+                    nc.scalar.activation(
+                        out=tanh_g[:],
+                        in_=own[:, 2 * half + s, :],
+                        func=ACT.Tanh,
+                        accum_out=sums[:, column : column + 1],
+                    )
+
+        for pair in range(ROW_TILES // 2):
+            make_l(pair)
+        quantise_m(0)
+        prepare_r()
+        for g2 in range(PASSES):
+            if g2 + 2 < PASSES:
+                m_raw_of[g2 + 2] = load_m(g2 + 2)
+            if g2 + 1 < PASSES:
+                quantise_m(g2 + 1)
+            for rt in range(ROW_TILES):
+                make_u(g2, rt)
+                bank = g2 * ROW_TILES + rt
+                for unit in range(bank * R_UNITS_PER_BANK, min((bank + 1) * R_UNITS_PER_BANK, PASSES * C)):
+                    make_r_unit(unit // C, unit % C)
+                if g2 == PASSES - 1 and rt % 2 == 0 and rt > 0:
+                    make_sums(rt // 2 - 1)
+        make_sums(ROW_TILES // 2 - 1)
+
+        Q = 2 * ROW_TILES
+        sums_t = psum.tile([P, P], F32, tag="bank")
+        nc.tensor.transpose(out=sums_t[:], in_=sums[:], identity=ident_f32[:])
+        by_batch = sums_t[0:Q, :].rearrange("q (c l) -> q l c", l=TILE_B)
+        top = small.tile([Q, TILE_B], F32)
+        nc.vector.tensor_reduce(out=top[:], in_=by_batch, axis=AX.X, op=ALU.max)
+        shifted = small.tile([Q, TILE_B, C], F32)
+        nc.vector.tensor_tensor(
+            out=shifted[:], in0=by_batch, in1=top[:].unsqueeze(2).to_broadcast([Q, TILE_B, C]), op=ALU.subtract
+        )
+        grown = small.tile([Q, TILE_B, C], F32)
+        nc.scalar.activation(out=grown[:], in_=shifted[:], func=ACT.Exp)
+        total = small.tile([Q, TILE_B], F32)
+        nc.vector.tensor_reduce(out=total[:], in_=grown[:], axis=AX.X, op=ALU.add)
+        share = small.tile([Q, TILE_B], F32)
+        nc.vector.reciprocal(out=share[:], in_=total[:])
+        gated = small.tile([Q, TILE_B, C], F32)
+        nc.vector.tensor_tensor(out=gated[:], in0=grown[:], in1=h_out[:], op=ALU.mult)
+        result = small.tile([Q, TILE_B, C], F32)
+        nc.vector.tensor_tensor(
+            out=result[:], in0=gated[:], in1=share[:].unsqueeze(2).to_broadcast([Q, TILE_B, C]), op=ALU.mult
+        )
+        for s in range(2):
+            nc.sync.dma_start(
+                out=out[:, s * C : (s + 1) * C].rearrange("(r l) c -> r l c", l=TILE_B),
+                in_=result[s * ROW_TILES : (s + 1) * ROW_TILES, :, :],
+            )

@@ -24,7 +24,10 @@ TILE_B = P // C
 ROW_TILES = B // TILE_B
 ROWS = B * C
 CHUNK = K_PASS
-R_UNITS_PER_BANK = 3
+R_UNITS_PER_BANK = 2
+
+BANKS = PASSES * ROW_TILES
+U_LAG = 3
 
 FLOPS = 2 * ROWS * E * E + 2 * B * C * C * E
 
@@ -36,20 +39,26 @@ def tile_mlp_embedding_layer_pa_kernel(tc, h_towers, W_emb, b_emb, M, out):
         keep = ctx.enter_context(tc.tile_pool(name="keep", bufs=1))
         m_in = ctx.enter_context(tc.tile_pool(name="m_in", bufs=2))
         m_words = ctx.enter_context(tc.tile_pool(name="m_words", bufs=3))
-        wide = ctx.enter_context(tc.tile_pool(name="wide", bufs=4))
-        work = ctx.enter_context(tc.tile_pool(name="work", bufs=4))
+        wide = ctx.enter_context(tc.tile_pool(name="wide", bufs=6))
+        work = ctx.enter_context(tc.tile_pool(name="work", bufs=2))
+        u_out = ctx.enter_context(tc.tile_pool(name="u_out", bufs=8))
         small = ctx.enter_context(tc.tile_pool(name="small", bufs=1))
         psum = ctx.enter_context(tc.psum_pool(name="psum", bufs=8))
+        ctx.enter_context(tc.manual_schedule())
 
-        def load_m(chunk):
+        def load_m(chunk, pieces):
             m_raw = m_in.tile([P, SLOTS, CHUNK], BF16)
-            nc.sync.dma_start(
-                out=m_raw[:],
-                in_=M.rearrange("(a p) n -> p a n", p=P)[:, :, chunk * CHUNK : (chunk + 1) * CHUNK],
-            )
+            step = SLOTS // pieces
+            for i in range(pieces):
+                nc.sync.dma_start(
+                    out=m_raw[:, i * step : (i + 1) * step, :],
+                    in_=M.rearrange("(a p) n -> p a n", p=P)[
+                        :, i * step : (i + 1) * step, chunk * CHUNK : (chunk + 1) * CHUNK
+                    ],
+                )
             return m_raw
 
-        m_raw_of = {0: load_m(0)}
+        m_raw_of = {0: load_m(0, 2)}
 
         h_all = const.tile([P, B, 2 * C], BF16)
         nc.scalar.dma_start(
@@ -64,11 +73,15 @@ def tile_mlp_embedding_layer_pa_kernel(tc, h_towers, W_emb, b_emb, M, out):
                 first = 64 * w + C * t
                 nc.scalar.dma_start(out=emb_l[first : first + C, :, :], in_=runs[t])
 
-        m_raw_of[1] = load_m(1)
+        ident_bf = const.tile([P, P], BF16)
+        make_identity(nc, ident_bf[:])
 
         emb_rows = const.tile([P, E], BF16)
-        nc.sync.dma_start(out=emb_rows[0 : 2 * C, :], in_=W_emb)
-        nc.sync.dma_start(out=emb_rows[2 * C : 4 * C, :], in_=b_emb)
+        nc.vector.memset(emb_rows[64:128, :], 0.0)
+        nc.gpsimd.dma_start(out=emb_rows[0 : 2 * C, :], in_=W_emb)
+        nc.gpsimd.dma_start(out=emb_rows[2 * C : 4 * C, :], in_=b_emb)
+
+        m_raw_of[1] = load_m(1, 1)
 
         h_out = small.tile([2 * ROW_TILES, TILE_B, C], BF16)
         for s in range(2):
@@ -77,8 +90,6 @@ def tile_mlp_embedding_layer_pa_kernel(tc, h_towers, W_emb, b_emb, M, out):
                 in_=h_towers[:, s * C : (s + 1) * C].rearrange("(r l) c -> r l c", l=TILE_B),
             )
 
-        ident_bf = const.tile([P, P], BF16)
-        make_identity(nc, ident_bf[:])
         ident_f32 = const.tile([P, P], F32)
         make_identity(nc, ident_f32[:])
 
@@ -90,16 +101,8 @@ def tile_mlp_embedding_layer_pa_kernel(tc, h_towers, W_emb, b_emb, M, out):
             op=ALU.add,
         )
 
-        same_l = const.tile([P, TILE_B], F32)
-        nc.vector.tensor_reduce(
-            out=same_l[:], in_=ident_f32[:].rearrange("p (c l) -> p l c", l=TILE_B), axis=AX.X, op=ALU.add
-        )
-        same_batch = const.tile([P, C, TILE_B], F32)
-        nc.vector.tensor_copy(out=same_batch[:], in_=same_l[:].unsqueeze(1).to_broadcast([P, C, TILE_B]))
-
         sums = small.tile([P, P], F32)
         nc.gpsimd.memset(sums[:], 0.0)
-        nc.gpsimd.memset(emb_rows[64:128, :], 0.0)
 
         m_codes = keep.tile([P, PASSES, E], U32, align_bytes=64)
         m_scales = keep.tile([P, PASSES, E], U8, align_bytes=64)
@@ -110,76 +113,94 @@ def tile_mlp_embedding_layer_pa_kernel(tc, h_towers, W_emb, b_emb, M, out):
         r_codes = keep.tile([P, PASSES, ROWS], U32, align_bytes=64)
         r_scales = keep.tile([P, PASSES, ROWS], U8, align_bytes=64)
 
-        spread = const.tile([P, ROW_TILES, C, TILE_B, PACK], BF16)
+        spread = wide.tile([P, ROW_TILES, C, TILE_B, PACK], BF16, tag="wide", align_bytes=64)
         for rt in range(ROW_TILES):
             nc.vector.tensor_copy(
                 out=spread[64:128, rt],
                 in_=pick[64:128].unsqueeze(2).to_broadcast([64, C, TILE_B, PACK]),
             )
 
-        def make_l(pair):
-            for rt in (2 * pair, 2 * pair + 1):
-                nc.vector.tensor_tensor(
-                    out=spread[0:64, rt],
-                    in0=h_all[0:64, rt * TILE_B : (rt + 1) * TILE_B, 0:C]
-                    .rearrange("p l c -> p c l")
-                    .unsqueeze(3)
-                    .to_broadcast([64, C, TILE_B, PACK]),
-                    in1=pick[0:64].unsqueeze(2).to_broadcast([64, C, TILE_B, PACK]),
-                    op=ALU.mult,
+        def spread_h(rt):
+            nc.vector.tensor_tensor(
+                out=spread[0:64, rt],
+                in0=h_all[0:64, rt * TILE_B : (rt + 1) * TILE_B, 0:C]
+                .rearrange("p l c -> p c l")
+                .unsqueeze(3)
+                .to_broadcast([64, C, TILE_B, PACK]),
+                in1=pick[0:64].unsqueeze(2).to_broadcast([64, C, TILE_B, PACK]),
+                op=ALU.mult,
+            )
+
+        l_bf_of = {}
+
+        def make_l(pair, g):
+            if g == 0:
+                l_bf_of[pair] = wide.tile([P, PASSES, 2 * K_PASS], BF16, tag="wide", name="l_bf", align_bytes=64)
+            l_bank = psum.tile([P, 2, K_PASS], BF16, tag="bank")
+            for half in range(2):
+                nc.tensor.matmul(
+                    out=l_bank[:, half, :],
+                    lhsT=emb_l[:, g, :],
+                    rhs=spread[:, 2 * pair + half].rearrange("p c l t -> p (c l t)"),
+                    start=True,
+                    stop=True,
                 )
-            l_bf = wide.tile([P, PASSES, 2 * K_PASS], BF16, tag="wide", align_bytes=64)
-            for g in range(PASSES):
-                l_bank = psum.tile([P, 2, K_PASS], BF16, tag="bank")
-                for half in range(2):
-                    nc.tensor.matmul(
-                        out=l_bank[:, half, :],
-                        lhsT=emb_l[:, g, :],
-                        rhs=spread[:, 2 * pair + half].rearrange("p c l t -> p (c l t)"),
-                        start=True,
-                        stop=True,
-                    )
-                nc.scalar.copy(out=l_bf[:, g, :], in_=l_bank[:].rearrange("p h w -> p (h w)"))
+            nc.scalar.copy(out=l_bf_of[pair][:, g, :], in_=l_bank[:].rearrange("p h w -> p (h w)"))
+
+        def quantise_l(pair):
             nc.vector.quantize_mx(
                 out=l_codes[:, pair].rearrange("p g w -> p (g w)").bitcast(FP8X4),
                 scales=l_scales[:, pair].rearrange("p g w -> p (g w)"),
-                in_=l_bf[:].rearrange("p g w -> p (g w)"),
+                in_=l_bf_of[pair][:].rearrange("p g w -> p (g w)"),
             )
 
-        def quantise_m(chunk):
-            m_raw = m_raw_of[chunk]
+        m_bf_of = {}
+
+        def regroup_m(chunk, g):
+            m_bf_of[g] = m_words.tile([P, CHUNK, PACK], BF16, name="m_bf", align_bytes=64)
+            nc.vector.tensor_copy(
+                out=m_bf_of[g][:].rearrange("p (c i) t -> p c t i", i=4),
+                in_=m_raw_of[chunk][:, g * PACK : (g + 1) * PACK, :].rearrange("p t (c i) -> p c t i", i=4),
+            )
+
+        def quantise_m(chunk, g):
             cols = slice(chunk * CHUNK, (chunk + 1) * CHUNK)
-            for g in range(PASSES):
-                m_bf = m_words.tile([P, CHUNK, PACK], BF16, align_bytes=64)
-                nc.vector.tensor_copy(
-                    out=m_bf[:].rearrange("p (c i) t -> p c t i", i=4),
-                    in_=m_raw[:, g * PACK : (g + 1) * PACK, :].rearrange("p t (c i) -> p c t i", i=4),
-                )
-                nc.vector.quantize_mx(
-                    out=m_codes[:, g, cols].bitcast(FP8X4),
-                    scales=m_scales[:, g, cols],
-                    in_=m_bf[:].rearrange("p n t -> p (n t)"),
-                )
+            nc.vector.quantize_mx(
+                out=m_codes[:, g, cols].bitcast(FP8X4),
+                scales=m_scales[:, g, cols],
+                in_=m_bf_of[g][:].rearrange("p n t -> p (n t)"),
+            )
 
         emb_t = const.tile([P, SLOTS, 4 * C], F32)
         h_right = const.tile([P, C, B], BF16)
 
-        def prepare_r():
+        t_bank_of = {}
+
+        def transpose_tables():
             for half in range(2):
-                t_bank = psum.tile([P, SLOTS // 2, P], BF16, tag="bank")
+                t_bank_of[half] = psum.tile([P, SLOTS // 2, P], BF16, tag="bank", name="t_bank")
                 for i in range(SLOTS // 2):
                     a = half * (SLOTS // 2) + i
-                    nc.tensor.transpose(out=t_bank[:, i, :], in_=emb_rows[:, a * P : (a + 1) * P], identity=ident_bf[:])
-                nc.vector.tensor_copy(
-                    out=emb_t[:, half * (SLOTS // 2) : (half + 1) * (SLOTS // 2), :], in_=t_bank[:, :, 0 : 4 * C]
+                    nc.tensor.transpose(
+                        out=t_bank_of[half][:, i, :], in_=emb_rows[:, a * P : (a + 1) * P], identity=ident_bf[:]
+                    )
+
+        def prepare_r():
+            for half in range(2):
+                nc.scalar.copy(
+                    out=emb_t[:, half * (SLOTS // 2) : (half + 1) * (SLOTS // 2), :],
+                    in_=t_bank_of[half][:, :, 0 : 4 * C],
                 )
-            nc.gpsimd.tensor_copy(out=h_right[:], in_=h_all[:, :, C : 2 * C].rearrange("p b c -> p c b"))
+            nc.scalar.copy(out=h_right[:], in_=h_all[:, :, C : 2 * C].rearrange("p b c -> p c b"))
 
         r_parts_of = {}
 
-        def make_r_unit(g, j):
+        def make_r_unit(unit):
+            g, j = unit // C, unit % C
             if j == 0:
-                r_parts_of[g] = wide.tile([P, ROW_TILES, C, PACK, TILE_B], BF16, tag="wide", name="r_parts", align_bytes=64)
+                r_parts_of[g] = wide.tile(
+                    [P, ROW_TILES, C, PACK, TILE_B], BF16, tag="wide", name="r_parts", align_bytes=64
+                )
             for t in range(PACK):
                 a = g * PACK + t
                 nc.scalar.activation(
@@ -189,17 +210,19 @@ def tile_mlp_embedding_layer_pa_kernel(tc, h_towers, W_emb, b_emb, M, out):
                     scale=emb_t[:, a, C + j : C + j + 1],
                     bias=emb_t[:, a, 3 * C + j : 3 * C + j + 1],
                 )
-            if j == C - 1:
-                r_bf = wide.tile([P, ROW_TILES * C, TILE_B, PACK], BF16, tag="wide", align_bytes=64)
-                nc.vector.tensor_copy(out=r_bf[:], in_=r_parts_of[g][:].rearrange("p r j t l -> p (r j) l t"))
-                nc.vector.quantize_mx(
-                    out=r_codes[:, g, :].bitcast(FP8X4),
-                    scales=r_scales[:, g, :],
-                    in_=r_bf[:].rearrange("p a l t -> p (a l t)"),
-                )
+
+        def quantise_r(g):
+            r_bf = wide.tile([P, ROW_TILES * C, TILE_B, PACK], BF16, tag="wide", align_bytes=64)
+            nc.vector.tensor_copy(out=r_bf[:], in_=r_parts_of[g][:].rearrange("p r j t l -> p (r j) l t"))
+            nc.vector.quantize_mx(
+                out=r_codes[:, g, :].bitcast(FP8X4),
+                scales=r_scales[:, g, :],
+                in_=r_bf[:].rearrange("p a l t -> p (a l t)"),
+            )
+
+        u_bf_of = {}
 
         def make_u(g2, rt):
-            rows = slice(rt * P, (rt + 1) * P)
             l_rows = slice((rt % 2) * P, (rt % 2 + 1) * P)
             u_bank = psum.tile([P, PACK, P], F32, tag="bank")
             for t in range(PACK):
@@ -214,13 +237,19 @@ def tile_mlp_embedding_layer_pa_kernel(tc, h_towers, W_emb, b_emb, M, out):
                         start=(g == 0),
                         stop=(g == PASSES - 1),
                     )
-            u_bf = work.tile([P, P, PACK], BF16, align_bytes=64)
-            nc.scalar.copy(out=u_bf[:], in_=u_bank[:].rearrange("p t r -> p r t"))
+            u_bf_of[(g2, rt)] = u_out.tile([P, P, PACK], BF16, name="u_bf", align_bytes=64)
+            nc.scalar.copy(out=u_bf_of[(g2, rt)][:], in_=u_bank[:].rearrange("p t r -> p r t"))
+
+        def quantise_u(g2, rt):
+            rows = slice(rt * P, (rt + 1) * P)
             nc.vector.quantize_mx(
                 out=u_codes[:, g2, rows].bitcast(FP8X4),
                 scales=u_scales[:, g2, rows],
-                in_=u_bf[:].rearrange("p r t -> p (r t)"),
+                in_=u_bf_of[(g2, rt)][:].rearrange("p r t -> p (r t)"),
             )
+
+        same_l = const.tile([P, TILE_B], F32)
+        same_batch = const.tile([P, C, TILE_B], F32)
 
         def make_sums(pair):
             g_bank = psum.tile([P, 4, P], F32, tag="bank")
@@ -257,23 +286,52 @@ def tile_mlp_embedding_layer_pa_kernel(tc, h_towers, W_emb, b_emb, M, out):
                         accum_out=sums[:, column : column + 1],
                     )
 
+        transpose_tables()
         for pair in range(ROW_TILES // 2):
-            make_l(pair)
-        quantise_m(0)
-        prepare_r()
-        for g2 in range(PASSES):
-            if g2 + 2 < PASSES:
-                m_raw_of[g2 + 2] = load_m(g2 + 2)
-            if g2 + 1 < PASSES:
-                quantise_m(g2 + 1)
-            for rt in range(ROW_TILES):
+            regroup_m(0, pair)
+            spread_h(2 * pair)
+            spread_h(2 * pair + 1)
+            if pair == 0:
+                prepare_r()
+            else:
+                quantise_m(0, pair - 1)
+            for g in range(PASSES):
+                make_l(pair, g)
+                make_r_unit(pair * PASSES + g)
+        quantise_m(0, PASSES - 1)
+        quantise_l(0)
+        quantise_l(1)
+
+        nc.vector.tensor_reduce(
+            out=same_l[:], in_=ident_f32[:].rearrange("p (c l) -> p l c", l=TILE_B), axis=AX.X, op=ALU.add
+        )
+        nc.vector.tensor_copy(out=same_batch[:], in_=same_l[:].unsqueeze(1).to_broadcast([P, C, TILE_B]))
+
+        for bank in range(BANKS + U_LAG):
+            g2, rt = bank // ROW_TILES, bank % ROW_TILES
+            if bank < BANKS:
+                if rt == 0 and g2 + 2 < PASSES:
+                    m_raw_of[g2 + 2] = load_m(g2 + 2, 1)
+                first_unit = C + bank * R_UNITS_PER_BANK
+                for unit in range(first_unit, min(first_unit + R_UNITS_PER_BANK, PASSES * C)):
+                    make_r_unit(unit)
                 make_u(g2, rt)
-                bank = g2 * ROW_TILES + rt
-                for unit in range(bank * R_UNITS_PER_BANK, min((bank + 1) * R_UNITS_PER_BANK, PASSES * C)):
-                    make_r_unit(unit // C, unit % C)
-                if g2 == PASSES - 1 and rt % 2 == 0 and rt > 0:
-                    make_sums(rt // 2 - 1)
-        make_sums(ROW_TILES // 2 - 1)
+                if g2 == 0 and rt < 2:
+                    quantise_l(2 + rt)
+                if g2 + 1 < PASSES and rt < PASSES:
+                    regroup_m(g2 + 1, rt)
+                    if rt > 0:
+                        quantise_m(g2 + 1, rt - 1)
+                if g2 + 1 < PASSES and rt == PASSES:
+                    quantise_m(g2 + 1, PASSES - 1)
+                if 0 < g2 < PASSES - 1 and rt == PASSES + 1:
+                    quantise_r(g2 - 1)
+                if g2 == PASSES - 1 and rt in (0, 2):
+                    quantise_r(PASSES - 2 + rt // 2)
+            if bank >= U_LAG:
+                quantise_u((bank - U_LAG) // ROW_TILES, (bank - U_LAG) % ROW_TILES)
+        for pair in range(ROW_TILES // 2):
+            make_sums(pair)
 
         Q = 2 * ROW_TILES
         sums_t = psum.tile([P, P], F32, tag="bank")

@@ -19,15 +19,15 @@ B = 64
 C = 16
 E = 2048
 PASSES = E // K_PASS
-SLOTS = E // P
 TILE_B = P // C
 ROW_TILES = B // TILE_B
+PAIRS = ROW_TILES // 2
 ROWS = B * C
 CHUNK = K_PASS
-R_UNITS_PER_BANK = 2
-
 BANKS = PASSES * ROW_TILES
 U_LAG = 3
+LEFT, RIGHT = 0, 1
+TENSOR_R_PASSES = 2
 
 FLOPS = 2 * ROWS * E * E + 2 * B * C * C * E
 
@@ -39,7 +39,7 @@ def tile_mlp_embedding_layer_pa_kernel(tc, h_towers, W_emb, b_emb, M, out):
         keep = ctx.enter_context(tc.tile_pool(name="keep", bufs=1))
         m_in = ctx.enter_context(tc.tile_pool(name="m_in", bufs=2))
         m_words = ctx.enter_context(tc.tile_pool(name="m_words", bufs=3))
-        wide = ctx.enter_context(tc.tile_pool(name="wide", bufs=6))
+        wide = ctx.enter_context(tc.tile_pool(name="wide", bufs=5))
         work = ctx.enter_context(tc.tile_pool(name="work", bufs=2))
         u_out = ctx.enter_context(tc.tile_pool(name="u_out", bufs=8))
         small = ctx.enter_context(tc.tile_pool(name="small", bufs=1))
@@ -47,8 +47,8 @@ def tile_mlp_embedding_layer_pa_kernel(tc, h_towers, W_emb, b_emb, M, out):
         ctx.enter_context(tc.manual_schedule())
 
         def load_m(chunk, pieces):
-            m_raw = m_in.tile([P, SLOTS, CHUNK], BF16)
-            step = SLOTS // pieces
+            m_raw = m_in.tile([P, PASSES * PACK, CHUNK], BF16)
+            step = PASSES * PACK // pieces
             for i in range(pieces):
                 nc.sync.dma_start(
                     out=m_raw[:, i * step : (i + 1) * step, :],
@@ -66,20 +66,17 @@ def tile_mlp_embedding_layer_pa_kernel(tc, h_towers, W_emb, b_emb, M, out):
             in_=h_towers.rearrange("b c -> (b c)").partition_broadcast(P),
         )
 
-        emb_l = const.tile([P, PASSES, P], BF16)
+        emb_k = const.tile([P, 2 * PASSES, P], BF16)
         for w, table in enumerate((W_emb, b_emb)):
-            runs = table[0:C, :].rearrange("c (g t p) -> t c g p", t=PACK, p=P)
-            for t in range(PACK):
-                first = 64 * w + C * t
-                nc.scalar.dma_start(out=emb_l[first : first + C, :, :], in_=runs[t])
+            runs = table.rearrange("c (a i p) -> i c a p", i=2, p=P)
+            for i in range(2):
+                first = 64 * w + 2 * C * i
+                nc.scalar.dma_start(out=emb_k[first : first + 2 * C, :, :], in_=runs[i])
 
-        ident_bf = const.tile([P, P], BF16)
-        make_identity(nc, ident_bf[:])
-
-        emb_rows = const.tile([P, E], BF16)
-        nc.vector.memset(emb_rows[64:128, :], 0.0)
-        nc.gpsimd.dma_start(out=emb_rows[0 : 2 * C, :], in_=W_emb)
-        nc.gpsimd.dma_start(out=emb_rows[2 * C : 4 * C, :], in_=b_emb)
+        first_in = small.tile([P, 1], F32)
+        nc.vector.memset(first_in[:], 0.0)
+        first_out = small.tile([P, 1], F32)
+        nc.scalar.activation(out=first_out[:], in_=first_in[:], func=ACT.Tanh)
 
         m_raw_of[1] = load_m(1, 1)
 
@@ -90,14 +87,16 @@ def tile_mlp_embedding_layer_pa_kernel(tc, h_towers, W_emb, b_emb, M, out):
                 in_=h_towers[:, s * C : (s + 1) * C].rearrange("(r l) c -> r l c", l=TILE_B),
             )
 
+        ident_bf = const.tile([P, P], BF16)
+        make_identity(nc, ident_bf[:])
         ident_f32 = const.tile([P, P], F32)
         make_identity(nc, ident_f32[:])
 
-        pick = const.tile([P, C, PACK], BF16)
+        pick = const.tile([P, 2 * C, 2], BF16)
         nc.vector.tensor_tensor(
             out=pick[:],
-            in0=ident_bf[:, 0:64].rearrange("p (t c) -> p c t", t=PACK),
-            in1=ident_bf[:, 64:128].rearrange("p (t c) -> p c t", t=PACK),
+            in0=ident_bf[:, 0:64].rearrange("p (i c) -> p c i", i=2),
+            in1=ident_bf[:, 64:128].rearrange("p (i c) -> p c i", i=2),
             op=ALU.add,
         )
 
@@ -106,52 +105,105 @@ def tile_mlp_embedding_layer_pa_kernel(tc, h_towers, W_emb, b_emb, M, out):
 
         m_codes = keep.tile([P, PASSES, E], U32, align_bytes=64)
         m_scales = keep.tile([P, PASSES, E], U8, align_bytes=64)
-        l_codes = keep.tile([P, ROW_TILES // 2, PASSES, 2 * P], U32, align_bytes=64)
-        l_scales = keep.tile([P, ROW_TILES // 2, PASSES, 2 * P], U8, align_bytes=64)
+        l_codes = keep.tile([P, PAIRS, PASSES, 2 * P], U32, align_bytes=64)
+        l_scales = keep.tile([P, PAIRS, PASSES, 2 * P], U8, align_bytes=64)
         u_codes = keep.tile([P, PASSES, ROWS], U32, align_bytes=64)
         u_scales = keep.tile([P, PASSES, ROWS], U8, align_bytes=64)
         r_codes = keep.tile([P, PASSES, ROWS], U32, align_bytes=64)
         r_scales = keep.tile([P, PASSES, ROWS], U8, align_bytes=64)
 
-        spread = wide.tile([P, ROW_TILES, C, TILE_B, PACK], BF16, tag="wide", align_bytes=64)
-        for rt in range(ROW_TILES):
-            nc.vector.tensor_copy(
-                out=spread[64:128, rt],
-                in_=pick[64:128].unsqueeze(2).to_broadcast([64, C, TILE_B, PACK]),
-            )
+        spread_of = {}
+        for s in (LEFT, RIGHT):
+            spread_of[s] = const.tile([P, ROW_TILES, C, TILE_B, 2], BF16, name="spread%d" % s)
+            for rt in range(ROW_TILES):
+                nc.vector.tensor_copy(
+                    out=spread_of[s][64:128, rt],
+                    in_=pick[64:128, s * C : (s + 1) * C, :].unsqueeze(2).to_broadcast([64, C, TILE_B, 2]),
+                )
 
-        def spread_h(rt):
+        def spread_h(s, rt):
             nc.vector.tensor_tensor(
-                out=spread[0:64, rt],
-                in0=h_all[0:64, rt * TILE_B : (rt + 1) * TILE_B, 0:C]
+                out=spread_of[s][0:64, rt],
+                in0=h_all[0:64, rt * TILE_B : (rt + 1) * TILE_B, s * C : (s + 1) * C]
                 .rearrange("p l c -> p c l")
                 .unsqueeze(3)
-                .to_broadcast([64, C, TILE_B, PACK]),
-                in1=pick[0:64].unsqueeze(2).to_broadcast([64, C, TILE_B, PACK]),
+                .to_broadcast([64, C, TILE_B, 2]),
+                in1=pick[0:64, s * C : (s + 1) * C, :].unsqueeze(2).to_broadcast([64, C, TILE_B, 2]),
                 op=ALU.mult,
             )
+
+        def make_emb(s, pair, g, emb_bf):
+            e_bank = psum.tile([P, 2 * P, 2, 2], BF16, tag="bank")
+            for half in range(2):
+                nc.tensor.matmul(
+                    out=e_bank[:, :, half, :],
+                    lhsT=emb_k[:, 2 * g + half, :],
+                    rhs=spread_of[s][:, 2 * pair : 2 * pair + 2].rearrange("p r c l i -> p (r c l) i"),
+                    start=True,
+                    stop=True,
+                )
+            nc.scalar.copy(out=emb_bf, in_=e_bank[:].rearrange("p r h i -> p (r h i)"))
 
         l_bf_of = {}
 
         def make_l(pair, g):
             if g == 0:
                 l_bf_of[pair] = wide.tile([P, PASSES, 2 * K_PASS], BF16, tag="wide", name="l_bf", align_bytes=64)
-            l_bank = psum.tile([P, 2, K_PASS], BF16, tag="bank")
-            for half in range(2):
-                nc.tensor.matmul(
-                    out=l_bank[:, half, :],
-                    lhsT=emb_l[:, g, :],
-                    rhs=spread[:, 2 * pair + half].rearrange("p c l t -> p (c l t)"),
-                    start=True,
-                    stop=True,
-                )
-            nc.scalar.copy(out=l_bf_of[pair][:, g, :], in_=l_bank[:].rearrange("p h w -> p (h w)"))
+            make_emb(LEFT, pair, g, l_bf_of[pair][:, g, :])
 
         def quantise_l(pair):
             nc.vector.quantize_mx(
                 out=l_codes[:, pair].rearrange("p g w -> p (g w)").bitcast(FP8X4),
                 scales=l_scales[:, pair].rearrange("p g w -> p (g w)"),
                 in_=l_bf_of[pair][:].rearrange("p g w -> p (g w)"),
+            )
+
+        r_bf_of = {}
+
+        def make_r_on_tensor(g, pair):
+            if pair == 0:
+                r_bf_of[g] = wide.tile([P, PAIRS, 2 * K_PASS], BF16, tag="wide", name="r_bf", align_bytes=64)
+            make_emb(RIGHT, pair, g, r_bf_of[g][:, pair, :])
+
+        def quantise_r(g):
+            nc.vector.quantize_mx(
+                out=r_codes[:, g, :].bitcast(FP8X4),
+                scales=r_scales[:, g, :],
+                in_=r_bf_of[g][:].rearrange("p a w -> p (a w)"),
+            )
+
+        emb_t = const.tile([P, 2 * PASSES, P], F32)
+        h_right = const.tile([P, C, B], BF16)
+
+        def prepare_r_on_scalar():
+            t_bank = psum.tile([P, 2 * PASSES, P], BF16, tag="bank")
+            for a in range(2 * PASSES):
+                nc.tensor.transpose(out=t_bank[:, a, :], in_=emb_k[:, a, :], identity=ident_bf[:])
+            nc.scalar.copy(out=emb_t[:], in_=t_bank[:])
+            nc.scalar.copy(out=h_right[:], in_=h_all[:, :, C : 2 * C].rearrange("p b c -> p c b"))
+
+        r_parts_of = {}
+
+        def make_r_unit(g, j):
+            if j == 0:
+                r_parts_of[g] = wide.tile(
+                    [P, ROW_TILES, C, PACK, TILE_B], BF16, tag="wide", name="r_parts", align_bytes=64
+                )
+            for t in range(PACK):
+                column = 2 * C * (t % 2) + C + j
+                nc.scalar.activation(
+                    out=r_parts_of[g][:, :, j, t, :],
+                    in_=h_right[:, j, :].rearrange("p (r l) -> p r l", l=TILE_B),
+                    func=ACT.Identity,
+                    scale=emb_t[:, 2 * g + t // 2, column : column + 1],
+                    bias=emb_t[:, 2 * g + t // 2, 64 + column : 64 + column + 1],
+                )
+
+        def regroup_r(g):
+            r_bf_of[g] = wide.tile([P, PAIRS, 2 * K_PASS], BF16, tag="wide", name="r_bf", align_bytes=64)
+            nc.vector.tensor_copy(
+                out=r_bf_of[g][:].rearrange("p a (b l t) -> p (a b) l t", l=TILE_B, t=PACK),
+                in_=r_parts_of[g][:].rearrange("p r j t l -> p (r j) l t"),
             )
 
         m_bf_of = {}
@@ -169,55 +221,6 @@ def tile_mlp_embedding_layer_pa_kernel(tc, h_towers, W_emb, b_emb, M, out):
                 out=m_codes[:, g, cols].bitcast(FP8X4),
                 scales=m_scales[:, g, cols],
                 in_=m_bf_of[g][:].rearrange("p n t -> p (n t)"),
-            )
-
-        emb_t = const.tile([P, SLOTS, 4 * C], F32)
-        h_right = const.tile([P, C, B], BF16)
-
-        t_bank_of = {}
-
-        def transpose_tables():
-            for half in range(2):
-                t_bank_of[half] = psum.tile([P, SLOTS // 2, P], BF16, tag="bank", name="t_bank")
-                for i in range(SLOTS // 2):
-                    a = half * (SLOTS // 2) + i
-                    nc.tensor.transpose(
-                        out=t_bank_of[half][:, i, :], in_=emb_rows[:, a * P : (a + 1) * P], identity=ident_bf[:]
-                    )
-
-        def prepare_r():
-            for half in range(2):
-                nc.scalar.copy(
-                    out=emb_t[:, half * (SLOTS // 2) : (half + 1) * (SLOTS // 2), :],
-                    in_=t_bank_of[half][:, :, 0 : 4 * C],
-                )
-            nc.scalar.copy(out=h_right[:], in_=h_all[:, :, C : 2 * C].rearrange("p b c -> p c b"))
-
-        r_parts_of = {}
-
-        def make_r_unit(unit):
-            g, j = unit // C, unit % C
-            if j == 0:
-                r_parts_of[g] = wide.tile(
-                    [P, ROW_TILES, C, PACK, TILE_B], BF16, tag="wide", name="r_parts", align_bytes=64
-                )
-            for t in range(PACK):
-                a = g * PACK + t
-                nc.scalar.activation(
-                    out=r_parts_of[g][:, :, j, t, :],
-                    in_=h_right[:, j, :].rearrange("p (r l) -> p r l", l=TILE_B),
-                    func=ACT.Identity,
-                    scale=emb_t[:, a, C + j : C + j + 1],
-                    bias=emb_t[:, a, 3 * C + j : 3 * C + j + 1],
-                )
-
-        def quantise_r(g):
-            r_bf = wide.tile([P, ROW_TILES * C, TILE_B, PACK], BF16, tag="wide", align_bytes=64)
-            nc.vector.tensor_copy(out=r_bf[:], in_=r_parts_of[g][:].rearrange("p r j t l -> p (r j) l t"))
-            nc.vector.quantize_mx(
-                out=r_codes[:, g, :].bitcast(FP8X4),
-                scales=r_scales[:, g, :],
-                in_=r_bf[:].rearrange("p a l t -> p (a l t)"),
             )
 
         u_bf_of = {}
@@ -286,21 +289,22 @@ def tile_mlp_embedding_layer_pa_kernel(tc, h_towers, W_emb, b_emb, M, out):
                         accum_out=sums[:, column : column + 1],
                     )
 
-        transpose_tables()
-        for pair in range(ROW_TILES // 2):
+        prepare_r_on_scalar()
+        for pair in range(PAIRS):
             regroup_m(0, pair)
-            spread_h(2 * pair)
-            spread_h(2 * pair + 1)
-            if pair == 0:
-                prepare_r()
-            else:
+            spread_h(LEFT, 2 * pair)
+            spread_h(LEFT, 2 * pair + 1)
+            if pair > 0:
                 quantise_m(0, pair - 1)
             for g in range(PASSES):
                 make_l(pair, g)
-                make_r_unit(pair * PASSES + g)
         quantise_m(0, PASSES - 1)
         quantise_l(0)
         quantise_l(1)
+        for rt in range(ROW_TILES):
+            spread_h(RIGHT, rt)
+        for unit in range(TENSOR_R_PASSES * PAIRS):
+            make_r_on_tensor(unit // PAIRS, unit % PAIRS)
 
         nc.vector.tensor_reduce(
             out=same_l[:], in_=ident_f32[:].rearrange("p (c l) -> p l c", l=TILE_B), axis=AX.X, op=ALU.add
@@ -312,25 +316,28 @@ def tile_mlp_embedding_layer_pa_kernel(tc, h_towers, W_emb, b_emb, M, out):
             if bank < BANKS:
                 if rt == 0 and g2 + 2 < PASSES:
                     m_raw_of[g2 + 2] = load_m(g2 + 2, 1)
-                first_unit = C + bank * R_UNITS_PER_BANK
-                for unit in range(first_unit, min(first_unit + R_UNITS_PER_BANK, PASSES * C)):
-                    make_r_unit(unit)
+                if g2 < 2:
+                    make_r_unit(TENSOR_R_PASSES + g2, 2 * rt)
+                    make_r_unit(TENSOR_R_PASSES + g2, 2 * rt + 1)
                 make_u(g2, rt)
                 if g2 == 0 and rt < 2:
                     quantise_l(2 + rt)
                 if g2 + 1 < PASSES and rt < PASSES:
                     regroup_m(g2 + 1, rt)
-                    if rt > 0:
-                        quantise_m(g2 + 1, rt - 1)
-                if g2 + 1 < PASSES and rt == PASSES:
-                    quantise_m(g2 + 1, PASSES - 1)
-                if 0 < g2 < PASSES - 1 and rt == PASSES + 1:
-                    quantise_r(g2 - 1)
-                if g2 == PASSES - 1 and rt in (0, 2):
-                    quantise_r(PASSES - 2 + rt // 2)
+                if g2 + 1 < PASSES and 0 < rt <= PASSES:
+                    quantise_m(g2 + 1, rt - 1)
+                if g2 == 1 and rt >= 6:
+                    quantise_r(rt - 6)
+                if g2 == 3 and rt == 0:
+                    regroup_r(2)
+                if g2 == 3 and rt == 2:
+                    regroup_r(3)
+                    quantise_r(2)
+                if g2 == 3 and rt == 4:
+                    quantise_r(3)
             if bank >= U_LAG:
                 quantise_u((bank - U_LAG) // ROW_TILES, (bank - U_LAG) % ROW_TILES)
-        for pair in range(ROW_TILES // 2):
+        for pair in range(PAIRS):
             make_sums(pair)
 
         Q = 2 * ROW_TILES

@@ -60,11 +60,10 @@ def tile_mlp_embedding_layer_pa_kernel(tc, h_towers, W_emb, b_emb, M, out):
 
         m_raw_of = {0: load_m(0, 2)}
 
-        h_all = const.tile([P, B, 2 * C], BF16)
-        nc.scalar.dma_start(
-            out=h_all[:].rearrange("p b c -> p (b c)"),
-            in_=h_towers.rearrange("b c -> (b c)").partition_broadcast(P),
-        )
+        h_rows = const.tile([P, P], BF16)
+        nc.vector.memset(h_rows[:], 1.0)
+        for i in range(2):
+            nc.scalar.dma_start(out=h_rows[0:B, 2 * C * i : 2 * C * (i + 1)], in_=h_towers)
 
         emb_k = const.tile([P, 2 * PASSES, P], BF16)
         for w, table in enumerate((W_emb, b_emb)):
@@ -77,6 +76,12 @@ def tile_mlp_embedding_layer_pa_kernel(tc, h_towers, W_emb, b_emb, M, out):
         nc.vector.memset(first_in[:], 0.0)
         first_out = small.tile([P, 1], F32)
         nc.scalar.activation(out=first_out[:], in_=first_in[:], func=ACT.Tanh)
+
+        h_all = const.tile([P, B, 2 * C], BF16)
+        nc.scalar.dma_start(
+            out=h_all[:].rearrange("p b c -> p (b c)"),
+            in_=h_towers.rearrange("b c -> (b c)").partition_broadcast(P),
+        )
 
         m_raw_of[1] = load_m(1, 1)
 
@@ -112,23 +117,16 @@ def tile_mlp_embedding_layer_pa_kernel(tc, h_towers, W_emb, b_emb, M, out):
         r_codes = keep.tile([P, PASSES, ROWS], U32, align_bytes=64)
         r_scales = keep.tile([P, PASSES, ROWS], U8, align_bytes=64)
 
+        h_own = psum.tile([P, P], BF16, tag="bank")
         spread_of = {}
         for s in (LEFT, RIGHT):
             spread_of[s] = const.tile([P, ROW_TILES, C, TILE_B, 2], BF16, name="spread%d" % s)
-            for rt in range(ROW_TILES):
-                nc.vector.tensor_copy(
-                    out=spread_of[s][64:128, rt],
-                    in_=pick[64:128, s * C : (s + 1) * C, :].unsqueeze(2).to_broadcast([64, C, TILE_B, 2]),
-                )
 
         def spread_h(s, rt):
             nc.vector.tensor_tensor(
-                out=spread_of[s][0:64, rt],
-                in0=h_all[0:64, rt * TILE_B : (rt + 1) * TILE_B, s * C : (s + 1) * C]
-                .rearrange("p l c -> p c l")
-                .unsqueeze(3)
-                .to_broadcast([64, C, TILE_B, 2]),
-                in1=pick[0:64, s * C : (s + 1) * C, :].unsqueeze(2).to_broadcast([64, C, TILE_B, 2]),
+                out=spread_of[s][:, rt],
+                in0=h_own[:, rt * TILE_B : (rt + 1) * TILE_B].unsqueeze(1).unsqueeze(3).to_broadcast([P, C, TILE_B, 2]),
+                in1=pick[:, s * C : (s + 1) * C, :].unsqueeze(2).to_broadcast([P, C, TILE_B, 2]),
                 op=ALU.mult,
             )
 
@@ -254,46 +252,44 @@ def tile_mlp_embedding_layer_pa_kernel(tc, h_towers, W_emb, b_emb, M, out):
         same_l = const.tile([P, TILE_B], F32)
         same_batch = const.tile([P, C, TILE_B], F32)
 
-        def make_sums(pair):
-            g_bank = psum.tile([P, 4, P], F32, tag="bank")
-            for half in range(2):
-                rows = slice((2 * pair + half) * P, (2 * pair + half + 1) * P)
-                for s in range(2):
-                    on_part = (r_codes, r_scales) if s == 0 else (u_codes, u_scales)
-                    on_free = (u_codes, u_scales) if s == 0 else (r_codes, r_scales)
-                    for g in range(PASSES):
-                        nc.tensor.matmul_mx(
-                            out=g_bank[:, 2 * half + s, :],
-                            lhsT=on_part[0][:, g, rows].bitcast(FP8X4),
-                            lhsT_scale=on_part[1][:, g, rows],
-                            rhs=on_free[0][:, g, rows].bitcast(FP8X4),
-                            rhs_scale=on_free[1][:, g, rows],
-                            start=(g == 0),
-                            stop=(g == PASSES - 1),
-                        )
-            own = work.tile([P, 4, P], F32)
+        def make_sums(rt):
+            rows = slice(rt * P, (rt + 1) * P)
+            g_bank = psum.tile([P, 2, P], F32, tag="bank")
+            for s in range(2):
+                on_part = (r_codes, r_scales) if s == 0 else (u_codes, u_scales)
+                on_free = (u_codes, u_scales) if s == 0 else (r_codes, r_scales)
+                for g in range(PASSES):
+                    nc.tensor.matmul_mx(
+                        out=g_bank[:, s, :],
+                        lhsT=on_part[0][:, g, rows].bitcast(FP8X4),
+                        lhsT_scale=on_part[1][:, g, rows],
+                        rhs=on_free[0][:, g, rows].bitcast(FP8X4),
+                        rhs_scale=on_free[1][:, g, rows],
+                        start=(g == 0),
+                        stop=(g == PASSES - 1),
+                    )
+            own = work.tile([P, 2, P], F32)
             nc.vector.tensor_tensor(
                 out=own[:],
                 in0=g_bank[:],
-                in1=same_batch[:].rearrange("p c l -> p (c l)").unsqueeze(1).to_broadcast([P, 4, P]),
+                in1=same_batch[:].rearrange("p c l -> p (c l)").unsqueeze(1).to_broadcast([P, 2, P]),
                 op=ALU.mult,
             )
-            for half in range(2):
-                for s in range(2):
-                    column = s * ROW_TILES + 2 * pair + half
-                    tanh_g = work.tile([P, P], F32)
-                    nc.scalar.activation(
-                        out=tanh_g[:],
-                        in_=own[:, 2 * half + s, :],
-                        func=ACT.Tanh,
-                        accum_out=sums[:, column : column + 1],
-                    )
+            for s in range(2):
+                tanh_g = work.tile([P, P], F32)
+                nc.scalar.activation(
+                    out=tanh_g[:],
+                    in_=own[:, s, :],
+                    func=ACT.Tanh,
+                    accum_out=sums[:, s * ROW_TILES + rt : s * ROW_TILES + rt + 1],
+                )
 
-        prepare_r_on_scalar()
+        nc.tensor.transpose(out=h_own[:], in_=h_rows[:], identity=ident_bf[:])
+        for s in (LEFT, RIGHT):
+            for rt in range(ROW_TILES):
+                spread_h(s, rt)
         for pair in range(PAIRS):
             regroup_m(0, pair)
-            spread_h(LEFT, 2 * pair)
-            spread_h(LEFT, 2 * pair + 1)
             if pair > 0:
                 quantise_m(0, pair - 1)
             for g in range(PASSES):
@@ -301,10 +297,9 @@ def tile_mlp_embedding_layer_pa_kernel(tc, h_towers, W_emb, b_emb, M, out):
         quantise_m(0, PASSES - 1)
         quantise_l(0)
         quantise_l(1)
-        for rt in range(ROW_TILES):
-            spread_h(RIGHT, rt)
         for unit in range(TENSOR_R_PASSES * PAIRS):
             make_r_on_tensor(unit // PAIRS, unit % PAIRS)
+        prepare_r_on_scalar()
 
         nc.vector.tensor_reduce(
             out=same_l[:], in_=ident_f32[:].rearrange("p (c l) -> p l c", l=TILE_B), axis=AX.X, op=ALU.add
@@ -337,8 +332,8 @@ def tile_mlp_embedding_layer_pa_kernel(tc, h_towers, W_emb, b_emb, M, out):
                     quantise_r(3)
             if bank >= U_LAG:
                 quantise_u((bank - U_LAG) // ROW_TILES, (bank - U_LAG) % ROW_TILES)
-        for pair in range(PAIRS):
-            make_sums(pair)
+        for rt in range(ROW_TILES):
+            make_sums(rt)
 
         Q = 2 * ROW_TILES
         sums_t = psum.tile([P, P], F32, tag="bank")

@@ -58,19 +58,20 @@ def tile_mlp_embedding_layer_pa_kernel(tc, h_towers, W_emb, b_emb, M, out):
                 )
             return m_raw
 
-        m_raw_of = {0: load_m(0, 2)}
-
         h_rows = const.tile([P, P], BF16)
-        nc.vector.memset(h_rows[:], 1.0)
         for i in range(2):
-            nc.scalar.dma_start(out=h_rows[0:B, 2 * C * i : 2 * C * (i + 1)], in_=h_towers)
+            nc.sync.dma_start(out=h_rows[0:B, 2 * C * i : 2 * C * (i + 1)], in_=h_towers)
+        nc.vector.memset(h_rows[0:B, 4 * C : P], 1.0)
+        nc.vector.memset(h_rows[B:P, :], 1.0)
 
         emb_k = const.tile([P, 2 * PASSES, P], BF16)
         for w, table in enumerate((W_emb, b_emb)):
             runs = table.rearrange("c (a i p) -> i c a p", i=2, p=P)
             for i in range(2):
                 first = 64 * w + 2 * C * i
-                nc.scalar.dma_start(out=emb_k[first : first + 2 * C, :, :], in_=runs[i])
+                nc.sync.dma_start(out=emb_k[first : first + 2 * C, :, :], in_=runs[i])
+
+        m_raw_of = {0: load_m(0, 2)}
 
         first_in = small.tile([P, 1], F32)
         nc.vector.memset(first_in[:], 0.0)
@@ -78,7 +79,7 @@ def tile_mlp_embedding_layer_pa_kernel(tc, h_towers, W_emb, b_emb, M, out):
         nc.scalar.activation(out=first_out[:], in_=first_in[:], func=ACT.Tanh)
 
         h_all = const.tile([P, B, 2 * C], BF16)
-        nc.scalar.dma_start(
+        nc.sync.dma_start(
             out=h_all[:].rearrange("p b c -> p (b c)"),
             in_=h_towers.rearrange("b c -> (b c)").partition_broadcast(P),
         )
@@ -173,12 +174,11 @@ def tile_mlp_embedding_layer_pa_kernel(tc, h_towers, W_emb, b_emb, M, out):
         emb_t = const.tile([P, 2 * PASSES, P], F32)
         h_right = const.tile([P, C, B], BF16)
 
-        def prepare_r_on_scalar():
+        def transpose_tables():
             t_bank = psum.tile([P, 2 * PASSES, P], BF16, tag="bank")
             for a in range(2 * PASSES):
                 nc.tensor.transpose(out=t_bank[:, a, :], in_=emb_k[:, a, :], identity=ident_bf[:])
             nc.scalar.copy(out=emb_t[:], in_=t_bank[:])
-            nc.scalar.copy(out=h_right[:], in_=h_all[:, :, C : 2 * C].rearrange("p b c -> p c b"))
 
         r_parts_of = {}
 
@@ -285,6 +285,7 @@ def tile_mlp_embedding_layer_pa_kernel(tc, h_towers, W_emb, b_emb, M, out):
                 )
 
         nc.tensor.transpose(out=h_own[:], in_=h_rows[:], identity=ident_bf[:])
+        transpose_tables()
         for s in (LEFT, RIGHT):
             for rt in range(ROW_TILES):
                 spread_h(s, rt)
@@ -299,7 +300,7 @@ def tile_mlp_embedding_layer_pa_kernel(tc, h_towers, W_emb, b_emb, M, out):
         quantise_l(1)
         for unit in range(TENSOR_R_PASSES * PAIRS):
             make_r_on_tensor(unit // PAIRS, unit % PAIRS)
-        prepare_r_on_scalar()
+        nc.scalar.copy(out=h_right[:], in_=h_all[:, :, C : 2 * C].rearrange("p b c -> p c b"))
 
         nc.vector.tensor_reduce(
             out=same_l[:], in_=ident_f32[:].rearrange("p (c l) -> p l c", l=TILE_B), axis=AX.X, op=ALU.add

@@ -19,15 +19,16 @@ B = 64
 C = 16
 E = 2048
 PASSES = E // K_PASS
+RUNS = E // P
 TILE_B = P // C
 ROW_TILES = B // TILE_B
 PAIRS = ROW_TILES // 2
 ROWS = B * C
 CHUNK = K_PASS
 BANKS = PASSES * ROW_TILES
-U_LAG = 3
 LEFT, RIGHT = 0, 1
 TENSOR_R_PASSES = 2
+U_LAG = 3
 
 FLOPS = 2 * ROWS * E * E + 2 * B * C * C * E
 
@@ -46,37 +47,32 @@ def tile_mlp_embedding_layer_pa_kernel(tc, h_towers, W_emb, b_emb, M, out):
         psum = ctx.enter_context(tc.psum_pool(name="psum", bufs=8))
         ctx.enter_context(tc.manual_schedule())
 
-        def load_m(chunk, pieces):
-            m_raw = m_in.tile([P, PASSES * PACK, CHUNK], BF16)
-            step = PASSES * PACK // pieces
-            for i in range(pieces):
-                nc.sync.dma_start(
-                    out=m_raw[:, i * step : (i + 1) * step, :],
-                    in_=M.rearrange("(a p) n -> p a n", p=P)[
-                        :, i * step : (i + 1) * step, chunk * CHUNK : (chunk + 1) * CHUNK
-                    ],
-                )
-            return m_raw
-
         h_rows = const.tile([P, P], BF16)
         for i in range(2):
             nc.sync.dma_start(out=h_rows[0:B, 2 * C * i : 2 * C * (i + 1)], in_=h_towers)
         nc.vector.memset(h_rows[0:B, 4 * C : P], 1.0)
         nc.vector.memset(h_rows[B:P, :], 1.0)
 
-        emb_k = const.tile([P, 2 * PASSES, P], BF16)
+        tables = const.tile([P, RUNS // 2, P], BF16)
         for w, table in enumerate((W_emb, b_emb)):
-            runs = table.rearrange("c (a i p) -> i c a p", i=2, p=P)
             for i in range(2):
                 first = 64 * w + 2 * C * i
-                nc.sync.dma_start(out=emb_k[first : first + 2 * C, :, :], in_=runs[i])
+                nc.sync.dma_start(
+                    out=tables[first : first + 2 * C, :, :],
+                    in_=table.rearrange("c (d i p) -> i c d p", i=2, p=P)[i],
+                )
 
-        m_raw_of = {0: load_m(0, 2)}
+        def load_m(chunk):
+            m_raw = m_in.tile([P, RUNS, CHUNK], BF16)
+            for half in range(2):
+                runs = slice(half * RUNS // 2, (half + 1) * RUNS // 2)
+                nc.sync.dma_start(
+                    out=m_raw[:, runs, :],
+                    in_=M.rearrange("(run p) n -> p run n", p=P)[:, runs, chunk * CHUNK : (chunk + 1) * CHUNK],
+                )
+            return m_raw
 
-        first_in = small.tile([P, 1], F32)
-        nc.vector.memset(first_in[:], 0.0)
-        first_out = small.tile([P, 1], F32)
-        nc.scalar.activation(out=first_out[:], in_=first_in[:], func=ACT.Tanh)
+        m_raw_of = {0: load_m(0), 1: load_m(1)}
 
         h_all = const.tile([P, B, 2 * C], BF16)
         nc.sync.dma_start(
@@ -84,14 +80,17 @@ def tile_mlp_embedding_layer_pa_kernel(tc, h_towers, W_emb, b_emb, M, out):
             in_=h_towers.rearrange("b c -> (b c)").partition_broadcast(P),
         )
 
-        m_raw_of[1] = load_m(1, 1)
-
         h_out = small.tile([2 * ROW_TILES, TILE_B, C], BF16)
-        for s in range(2):
+        for s in (LEFT, RIGHT):
             nc.sync.dma_start(
                 out=h_out[s * ROW_TILES : (s + 1) * ROW_TILES, :, :],
                 in_=h_towers[:, s * C : (s + 1) * C].rearrange("(r l) c -> r l c", l=TILE_B),
             )
+
+        first_in = small.tile([P, 1], F32)
+        nc.vector.memset(first_in[:], 0.0)
+        first_out = small.tile([P, 1], F32)
+        nc.scalar.activation(out=first_out[:], in_=first_in[:], func=ACT.Tanh)
 
         ident_bf = const.tile([P, P], BF16)
         make_identity(nc, ident_bf[:])
@@ -136,7 +135,7 @@ def tile_mlp_embedding_layer_pa_kernel(tc, h_towers, W_emb, b_emb, M, out):
             for half in range(2):
                 nc.tensor.matmul(
                     out=e_bank[:, :, half, :],
-                    lhsT=emb_k[:, 2 * g + half, :],
+                    lhsT=tables[:, 2 * g + half, :],
                     rhs=spread_of[s][:, 2 * pair : 2 * pair + 2].rearrange("p r c l i -> p (r c l) i"),
                     start=True,
                     stop=True,
@@ -171,18 +170,18 @@ def tile_mlp_embedding_layer_pa_kernel(tc, h_towers, W_emb, b_emb, M, out):
                 in_=r_bf_of[g][:].rearrange("p a w -> p (a w)"),
             )
 
-        emb_t = const.tile([P, 2 * PASSES, P], F32)
+        tables_t = const.tile([P, RUNS // 2, P], F32)
         h_right = const.tile([P, C, B], BF16)
 
         def transpose_tables():
-            t_bank = psum.tile([P, 2 * PASSES, P], BF16, tag="bank")
-            for a in range(2 * PASSES):
-                nc.tensor.transpose(out=t_bank[:, a, :], in_=emb_k[:, a, :], identity=ident_bf[:])
-            nc.scalar.copy(out=emb_t[:], in_=t_bank[:])
+            t_bank = psum.tile([P, RUNS // 2, P], BF16, tag="bank")
+            for d in range(RUNS // 2):
+                nc.tensor.transpose(out=t_bank[:, d, :], in_=tables[:, d, :], identity=ident_bf[:])
+            nc.scalar.copy(out=tables_t[:], in_=t_bank[:])
 
         r_parts_of = {}
 
-        def make_r_unit(g, j):
+        def make_r_on_scalar(g, j):
             if j == 0:
                 r_parts_of[g] = wide.tile(
                     [P, ROW_TILES, C, PACK, TILE_B], BF16, tag="wide", name="r_parts", align_bytes=64
@@ -193,8 +192,8 @@ def tile_mlp_embedding_layer_pa_kernel(tc, h_towers, W_emb, b_emb, M, out):
                     out=r_parts_of[g][:, :, j, t, :],
                     in_=h_right[:, j, :].rearrange("p (r l) -> p r l", l=TILE_B),
                     func=ACT.Identity,
-                    scale=emb_t[:, 2 * g + t // 2, column : column + 1],
-                    bias=emb_t[:, 2 * g + t // 2, 64 + column : 64 + column + 1],
+                    scale=tables_t[:, 2 * g + t // 2, column : column + 1],
+                    bias=tables_t[:, 2 * g + t // 2, 64 + column : 64 + column + 1],
                 )
 
         def regroup_r(g):
@@ -209,8 +208,8 @@ def tile_mlp_embedding_layer_pa_kernel(tc, h_towers, W_emb, b_emb, M, out):
         def regroup_m(chunk, g):
             m_bf_of[g] = m_words.tile([P, CHUNK, PACK], BF16, name="m_bf", align_bytes=64)
             nc.vector.tensor_copy(
-                out=m_bf_of[g][:].rearrange("p (c i) t -> p c t i", i=4),
-                in_=m_raw_of[chunk][:, g * PACK : (g + 1) * PACK, :].rearrange("p t (c i) -> p c t i", i=4),
+                out=m_bf_of[g][:].rearrange("p (c x) t -> p c t x", x=4),
+                in_=m_raw_of[chunk][:, g * PACK : (g + 1) * PACK, :].rearrange("p t (c x) -> p c t x", x=4),
             )
 
         def quantise_m(chunk, g):
@@ -223,11 +222,11 @@ def tile_mlp_embedding_layer_pa_kernel(tc, h_towers, W_emb, b_emb, M, out):
 
         u_bf_of = {}
 
-        def make_u(g2, rt):
+        def make_u(chunk, rt):
             l_rows = slice((rt % 2) * P, (rt % 2 + 1) * P)
             u_bank = psum.tile([P, PACK, P], F32, tag="bank")
             for t in range(PACK):
-                n_cols = slice((g2 * PACK + t) * P, (g2 * PACK + t + 1) * P)
+                n_cols = slice((chunk * PACK + t) * P, (chunk * PACK + t + 1) * P)
                 for g in range(PASSES):
                     nc.tensor.matmul_mx(
                         out=u_bank[:, t, :],
@@ -238,26 +237,32 @@ def tile_mlp_embedding_layer_pa_kernel(tc, h_towers, W_emb, b_emb, M, out):
                         start=(g == 0),
                         stop=(g == PASSES - 1),
                     )
-            u_bf_of[(g2, rt)] = u_out.tile([P, P, PACK], BF16, name="u_bf", align_bytes=64)
-            nc.scalar.copy(out=u_bf_of[(g2, rt)][:], in_=u_bank[:].rearrange("p t r -> p r t"))
+            u_bf_of[(chunk, rt)] = u_out.tile([P, P, PACK], BF16, name="u_bf", align_bytes=64)
+            nc.scalar.copy(out=u_bf_of[(chunk, rt)][:], in_=u_bank[:].rearrange("p t r -> p r t"))
 
-        def quantise_u(g2, rt):
+        def quantise_u(chunk, rt):
             rows = slice(rt * P, (rt + 1) * P)
             nc.vector.quantize_mx(
-                out=u_codes[:, g2, rows].bitcast(FP8X4),
-                scales=u_scales[:, g2, rows],
-                in_=u_bf_of[(g2, rt)][:].rearrange("p r t -> p (r t)"),
+                out=u_codes[:, chunk, rows].bitcast(FP8X4),
+                scales=u_scales[:, chunk, rows],
+                in_=u_bf_of[(chunk, rt)][:].rearrange("p r t -> p (r t)"),
             )
 
         same_l = const.tile([P, TILE_B], F32)
         same_batch = const.tile([P, C, TILE_B], F32)
 
+        def make_same_batch():
+            nc.vector.tensor_reduce(
+                out=same_l[:], in_=ident_f32[:].rearrange("p (c l) -> p l c", l=TILE_B), axis=AX.X, op=ALU.add
+            )
+            nc.vector.tensor_copy(out=same_batch[:], in_=same_l[:].unsqueeze(1).to_broadcast([P, C, TILE_B]))
+
         def make_sums(rt):
             rows = slice(rt * P, (rt + 1) * P)
             g_bank = psum.tile([P, 2, P], F32, tag="bank")
-            for s in range(2):
-                on_part = (r_codes, r_scales) if s == 0 else (u_codes, u_scales)
-                on_free = (u_codes, u_scales) if s == 0 else (r_codes, r_scales)
+            for s in (LEFT, RIGHT):
+                on_part = (r_codes, r_scales) if s == LEFT else (u_codes, u_scales)
+                on_free = (u_codes, u_scales) if s == LEFT else (r_codes, r_scales)
                 for g in range(PASSES):
                     nc.tensor.matmul_mx(
                         out=g_bank[:, s, :],
@@ -275,7 +280,7 @@ def tile_mlp_embedding_layer_pa_kernel(tc, h_towers, W_emb, b_emb, M, out):
                 in1=same_batch[:].rearrange("p c l -> p (c l)").unsqueeze(1).to_broadcast([P, 2, P]),
                 op=ALU.mult,
             )
-            for s in range(2):
+            for s in (LEFT, RIGHT):
                 tanh_g = work.tile([P, P], F32)
                 nc.scalar.activation(
                     out=tanh_g[:],
@@ -298,39 +303,36 @@ def tile_mlp_embedding_layer_pa_kernel(tc, h_towers, W_emb, b_emb, M, out):
         quantise_m(0, PASSES - 1)
         quantise_l(0)
         quantise_l(1)
-        for unit in range(TENSOR_R_PASSES * PAIRS):
-            make_r_on_tensor(unit // PAIRS, unit % PAIRS)
-        nc.scalar.copy(out=h_right[:], in_=h_all[:, :, C : 2 * C].rearrange("p b c -> p c b"))
-
-        nc.vector.tensor_reduce(
-            out=same_l[:], in_=ident_f32[:].rearrange("p (c l) -> p l c", l=TILE_B), axis=AX.X, op=ALU.add
-        )
-        nc.vector.tensor_copy(out=same_batch[:], in_=same_l[:].unsqueeze(1).to_broadcast([P, C, TILE_B]))
+        for g in range(TENSOR_R_PASSES):
+            for pair in range(PAIRS):
+                make_r_on_tensor(g, pair)
+        make_same_batch()
 
         for bank in range(BANKS + U_LAG):
-            g2, rt = bank // ROW_TILES, bank % ROW_TILES
+            chunk, rt = bank // ROW_TILES, bank % ROW_TILES
             if bank < BANKS:
-                if rt == 0 and g2 + 2 < PASSES:
-                    m_raw_of[g2 + 2] = load_m(g2 + 2, 1)
-                if g2 < 2:
-                    make_r_unit(TENSOR_R_PASSES + g2, 2 * rt)
-                    make_r_unit(TENSOR_R_PASSES + g2, 2 * rt + 1)
-                make_u(g2, rt)
-                if g2 == 0 and rt < 2:
+                if rt == 0 and chunk + 2 < PASSES:
+                    m_raw_of[chunk + 2] = load_m(chunk + 2)
+                if bank == ROW_TILES:
+                    nc.scalar.copy(out=h_right[:], in_=h_all[:, :, C : 2 * C].rearrange("p b c -> p c b"))
+                if chunk in (1, 2):
+                    make_r_on_scalar(TENSOR_R_PASSES + chunk - 1, 2 * rt)
+                    make_r_on_scalar(TENSOR_R_PASSES + chunk - 1, 2 * rt + 1)
+                make_u(chunk, rt)
+                if chunk == 0 and rt < 2:
                     quantise_l(2 + rt)
-                if g2 + 1 < PASSES and rt < PASSES:
-                    regroup_m(g2 + 1, rt)
-                if g2 + 1 < PASSES and 0 < rt <= PASSES:
-                    quantise_m(g2 + 1, rt - 1)
-                if g2 == 1 and rt >= 6:
-                    quantise_r(rt - 6)
-                if g2 == 3 and rt == 0:
-                    regroup_r(2)
-                if g2 == 3 and rt == 2:
-                    regroup_r(3)
-                    quantise_r(2)
-                if g2 == 3 and rt == 4:
-                    quantise_r(3)
+                if chunk + 1 < PASSES and rt < PASSES:
+                    regroup_m(chunk + 1, rt)
+                if chunk + 1 < PASSES and 0 < rt <= PASSES:
+                    quantise_m(chunk + 1, rt - 1)
+                if chunk == 1 and rt >= ROW_TILES - TENSOR_R_PASSES:
+                    quantise_r(rt - (ROW_TILES - TENSOR_R_PASSES))
+                if chunk == PASSES - 1 and rt % 2 == 0:
+                    g = TENSOR_R_PASSES + rt // 2
+                    if g < PASSES:
+                        regroup_r(g)
+                    if TENSOR_R_PASSES < g <= PASSES:
+                        quantise_r(g - 1)
             if bank >= U_LAG:
                 quantise_u((bank - U_LAG) // ROW_TILES, (bank - U_LAG) % ROW_TILES)
         for rt in range(ROW_TILES):
@@ -358,7 +360,7 @@ def tile_mlp_embedding_layer_pa_kernel(tc, h_towers, W_emb, b_emb, M, out):
         nc.vector.tensor_tensor(
             out=result[:], in0=gated[:], in1=share[:].unsqueeze(2).to_broadcast([Q, TILE_B, C]), op=ALU.mult
         )
-        for s in range(2):
+        for s in (LEFT, RIGHT):
             nc.sync.dma_start(
                 out=out[:, s * C : (s + 1) * C].rearrange("(r l) c -> r l c", l=TILE_B),
                 in_=result[s * ROW_TILES : (s + 1) * ROW_TILES, :, :],

@@ -26,6 +26,7 @@ PAIRS = ROW_TILES // 2
 ROWS = B * C
 CHUNK = K_PASS
 BANKS = PASSES * ROW_TILES
+TILES_IN_BANK = 4
 LEFT, RIGHT = 0, 1
 TENSOR_R_PASSES = 2
 U_LAG = 3
@@ -41,8 +42,9 @@ def tile_mlp_embedding_layer_pa_kernel(tc, h_towers, W_emb, b_emb, M, out):
         m_in = ctx.enter_context(tc.tile_pool(name="m_in", bufs=2))
         m_words = ctx.enter_context(tc.tile_pool(name="m_words", bufs=3))
         wide = ctx.enter_context(tc.tile_pool(name="wide", bufs=5))
-        work = ctx.enter_context(tc.tile_pool(name="work", bufs=2))
+        work = ctx.enter_context(tc.tile_pool(name="work", bufs=4))
         u_out = ctx.enter_context(tc.tile_pool(name="u_out", bufs=8))
+        tanh_pool = ctx.enter_context(tc.tile_pool(name="tanh_pool", bufs=8))
         small = ctx.enter_context(tc.tile_pool(name="small", bufs=1))
         psum = ctx.enter_context(tc.psum_pool(name="psum", bufs=8))
         ctx.enter_context(tc.manual_schedule())
@@ -257,37 +259,43 @@ def tile_mlp_embedding_layer_pa_kernel(tc, h_towers, W_emb, b_emb, M, out):
             )
             nc.vector.tensor_copy(out=same_batch[:], in_=same_l[:].unsqueeze(1).to_broadcast([P, C, TILE_B]))
 
-        def make_sums(rt):
+        tanh_of = {}
+
+        def make_g(rt):
             rows = slice(rt * P, (rt + 1) * P)
-            g_bank = psum.tile([P, 2, P], F32, tag="bank")
-            for s in (LEFT, RIGHT):
-                on_part = (r_codes, r_scales) if s == LEFT else (u_codes, u_scales)
-                on_free = (u_codes, u_scales) if s == LEFT else (r_codes, r_scales)
-                for g in range(PASSES):
-                    nc.tensor.matmul_mx(
-                        out=g_bank[:, s, :],
-                        lhsT=on_part[0][:, g, rows].bitcast(FP8X4),
-                        lhsT_scale=on_part[1][:, g, rows],
-                        rhs=on_free[0][:, g, rows].bitcast(FP8X4),
-                        rhs_scale=on_free[1][:, g, rows],
-                        start=(g == 0),
-                        stop=(g == PASSES - 1),
-                    )
-            own = work.tile([P, 2, P], F32)
-            nc.vector.tensor_tensor(
-                out=own[:],
-                in0=g_bank[:],
-                in1=same_batch[:].rearrange("p c l -> p (c l)").unsqueeze(1).to_broadcast([P, 2, P]),
-                op=ALU.mult,
-            )
-            for s in (LEFT, RIGHT):
-                tanh_g = work.tile([P, P], F32)
-                nc.scalar.activation(
-                    out=tanh_g[:],
-                    in_=own[:, s, :],
-                    func=ACT.Tanh,
-                    accum_out=sums[:, s * ROW_TILES + rt : s * ROW_TILES + rt + 1],
+            g_bank = psum.tile([P, P], F32, tag="bank")
+            for g in range(PASSES):
+                nc.tensor.matmul_mx(
+                    out=g_bank[:],
+                    lhsT=u_codes[:, g, rows].bitcast(FP8X4),
+                    lhsT_scale=u_scales[:, g, rows],
+                    rhs=r_codes[:, g, rows].bitcast(FP8X4),
+                    rhs_scale=r_scales[:, g, rows],
+                    start=(g == 0),
+                    stop=(g == PASSES - 1),
                 )
+            own = work.tile([P, P], F32)
+            nc.vector.tensor_tensor(
+                out=own[:], in0=g_bank[:], in1=same_batch[:].rearrange("p c l -> p (c l)"), op=ALU.mult
+            )
+            tanh_of[rt] = tanh_pool.tile([P, P], F32, name="tanh_g")
+            nc.scalar.activation(
+                out=tanh_of[rt][:],
+                in_=own[:],
+                func=ACT.Tanh,
+                accum_out=sums[:, RIGHT * ROW_TILES + rt : RIGHT * ROW_TILES + rt + 1],
+            )
+
+        def sum_over_i(first_rt):
+            turned = psum.tile([P, TILES_IN_BANK, P], F32, tag="bank")
+            for k in range(TILES_IN_BANK):
+                nc.tensor.transpose(out=turned[:, k, :], in_=tanh_of[first_rt + k][:], identity=ident_f32[:])
+            nc.vector.tensor_reduce(
+                out=sums[:, LEFT * ROW_TILES + first_rt : LEFT * ROW_TILES + first_rt + TILES_IN_BANK],
+                in_=turned[:],
+                axis=AX.X,
+                op=ALU.add,
+            )
 
         nc.tensor.transpose(out=h_own[:], in_=h_rows[:], identity=ident_bf[:])
         transpose_tables()
@@ -336,7 +344,9 @@ def tile_mlp_embedding_layer_pa_kernel(tc, h_towers, W_emb, b_emb, M, out):
             if bank >= U_LAG:
                 quantise_u((bank - U_LAG) // ROW_TILES, (bank - U_LAG) % ROW_TILES)
         for rt in range(ROW_TILES):
-            make_sums(rt)
+            make_g(rt)
+        for first_rt in range(0, ROW_TILES, TILES_IN_BANK):
+            sum_over_i(first_rt)
 
         Q = 2 * ROW_TILES
         sums_t = psum.tile([P, P], F32, tag="bank")

@@ -50,10 +50,10 @@ def tile_mlp_embedding_layer_pa_kernel(tc, h_towers, W_emb, b_emb, M, out):
         ctx.enter_context(tc.manual_schedule())
 
         h_rows = const.tile([P, P], BF16)
-        for i in range(2):
-            nc.sync.dma_start(out=h_rows[0:B, 2 * C * i : 2 * C * (i + 1)], in_=h_towers)
-        nc.vector.memset(h_rows[0:B, 4 * C : P], 1.0)
-        nc.vector.memset(h_rows[B:P, :], 1.0)
+        for twin in range(2):
+            for i in range(2):
+                nc.sync.dma_start(out=h_rows[twin:P:2, 2 * C * i : 2 * C * (i + 1)], in_=h_towers)
+        nc.vector.memset(h_rows[:, 4 * C : P], 1.0)
 
         tables = const.tile([P, RUNS // 2, P], BF16)
         for w, table in enumerate((W_emb, b_emb)):
@@ -66,8 +66,8 @@ def tile_mlp_embedding_layer_pa_kernel(tc, h_towers, W_emb, b_emb, M, out):
 
         def load_m(chunk):
             m_raw = m_in.tile([P, RUNS, CHUNK], BF16)
-            for half in range(2):
-                runs = slice(half * RUNS // 2, (half + 1) * RUNS // 2)
+            for g in range(PASSES):
+                runs = slice(g * PACK, (g + 1) * PACK)
                 nc.sync.dma_start(
                     out=m_raw[:, runs, :],
                     in_=M.rearrange("(run p) n -> p run n", p=P)[:, runs, chunk * CHUNK : (chunk + 1) * CHUNK],
@@ -99,11 +99,11 @@ def tile_mlp_embedding_layer_pa_kernel(tc, h_towers, W_emb, b_emb, M, out):
         ident_f32 = const.tile([P, P], F32)
         make_identity(nc, ident_f32[:])
 
-        pick = const.tile([P, 2 * C, 2], BF16)
+        pick = const.tile([P, 2 * C, TILE_B, 2], BF16)
         nc.vector.tensor_tensor(
             out=pick[:],
-            in0=ident_bf[:, 0:64].rearrange("p (i c) -> p c i", i=2),
-            in1=ident_bf[:, 64:128].rearrange("p (i c) -> p c i", i=2),
+            in0=ident_bf[:, 0:64].rearrange("p (i c) -> p c i", i=2).unsqueeze(2).to_broadcast([P, 2 * C, TILE_B, 2]),
+            in1=ident_bf[:, 64:128].rearrange("p (i c) -> p c i", i=2).unsqueeze(2).to_broadcast([P, 2 * C, TILE_B, 2]),
             op=ALU.add,
         )
 
@@ -119,16 +119,20 @@ def tile_mlp_embedding_layer_pa_kernel(tc, h_towers, W_emb, b_emb, M, out):
         r_codes = keep.tile([P, PASSES, ROWS], U32, align_bytes=64)
         r_scales = keep.tile([P, PASSES, ROWS], U8, align_bytes=64)
 
-        h_own = psum.tile([P, P], BF16, tag="bank")
+        h_own = psum.tile([P, B, 2], BF16, tag="bank")
         spread_of = {}
         for s in (LEFT, RIGHT):
             spread_of[s] = const.tile([P, ROW_TILES, C, TILE_B, 2], BF16, name="spread%d" % s)
 
-        def spread_h(s, rt):
+        def spread_h(s, pair):
+            shape = [P, 2, C, 2 * TILE_B]
             nc.vector.tensor_tensor(
-                out=spread_of[s][:, rt],
-                in0=h_own[:, rt * TILE_B : (rt + 1) * TILE_B].unsqueeze(1).unsqueeze(3).to_broadcast([P, C, TILE_B, 2]),
-                in1=pick[:, s * C : (s + 1) * C, :].unsqueeze(2).to_broadcast([P, C, TILE_B, 2]),
+                out=spread_of[s][:, 2 * pair : 2 * pair + 2].rearrange("p r c l i -> p r c (l i)"),
+                in0=h_own[:, 2 * pair * TILE_B : 2 * (pair + 1) * TILE_B, :]
+                .rearrange("p (r l) i -> p r (l i)", r=2)
+                .unsqueeze(2)
+                .to_broadcast(shape),
+                in1=pick[:, s * C : (s + 1) * C].rearrange("p c l i -> p c (l i)").unsqueeze(1).to_broadcast(shape),
                 op=ALU.mult,
             )
 
@@ -297,11 +301,11 @@ def tile_mlp_embedding_layer_pa_kernel(tc, h_towers, W_emb, b_emb, M, out):
                 op=ALU.add,
             )
 
-        nc.tensor.transpose(out=h_own[:], in_=h_rows[:], identity=ident_bf[:])
+        nc.tensor.transpose(out=h_own[:].rearrange("p b i -> p (b i)"), in_=h_rows[:], identity=ident_bf[:])
         transpose_tables()
         for s in (LEFT, RIGHT):
-            for rt in range(ROW_TILES):
-                spread_h(s, rt)
+            for pair in range(PAIRS):
+                spread_h(s, pair)
         for pair in range(PAIRS):
             regroup_m(0, pair)
             if pair > 0:

@@ -29,6 +29,8 @@ BANKS = PASSES * ROW_TILES
 TILES_IN_BANK = 4
 LEFT, RIGHT = 0, 1
 TENSOR_R_PASSES = 2
+SCALAR_R_UNITS = (PASSES - TENSOR_R_PASSES) * C
+SCALAR_R_BANKS = (PASSES - 1) * ROW_TILES
 U_LAG = 3
 
 FLOPS = 2 * ROWS * E * E + 2 * B * C * C * E
@@ -74,13 +76,14 @@ def tile_mlp_embedding_layer_pa_kernel(tc, h_towers, W_emb, b_emb, M, out):
                 )
             return m_raw
 
-        m_raw_of = {0: load_m(0), 1: load_m(1)}
+        m_raw_of = {0: load_m(0)}
 
         h_all = const.tile([P, B, 2 * C], BF16)
         nc.sync.dma_start(
             out=h_all[:].rearrange("p b c -> p (b c)"),
             in_=h_towers.rearrange("b c -> (b c)").partition_broadcast(P),
         )
+        m_raw_of[1] = load_m(1)
 
         h_out = small.tile([2 * ROW_TILES, TILE_B, C], BF16)
         for s in (LEFT, RIGHT):
@@ -325,11 +328,11 @@ def tile_mlp_embedding_layer_pa_kernel(tc, h_towers, W_emb, b_emb, M, out):
             if bank < BANKS:
                 if rt == 0 and chunk + 2 < PASSES:
                     m_raw_of[chunk + 2] = load_m(chunk + 2)
-                if bank == ROW_TILES:
+                if bank == 0:
                     nc.scalar.copy(out=h_right[:], in_=h_all[:, :, C : 2 * C].rearrange("p b c -> p c b"))
-                if chunk in (1, 2):
-                    make_r_on_scalar(TENSOR_R_PASSES + chunk - 1, 2 * rt)
-                    make_r_on_scalar(TENSOR_R_PASSES + chunk - 1, 2 * rt + 1)
+                for unit in range(SCALAR_R_UNITS):
+                    if unit * SCALAR_R_BANKS // SCALAR_R_UNITS == bank:
+                        make_r_on_scalar(TENSOR_R_PASSES + unit // C, unit % C)
                 make_u(chunk, rt)
                 if chunk == 0 and rt < 2:
                     quantise_l(2 + rt)

@@ -52,10 +52,10 @@ def tile_mlp_embedding_layer_pa_kernel(tc, h_towers, W_emb, b_emb, M, out):
         ctx.enter_context(tc.manual_schedule())
 
         h_rows = const.tile([P, P], BF16)
-        for twin in range(2):
-            for i in range(2):
-                nc.sync.dma_start(out=h_rows[twin:P:2, 2 * C * i : 2 * C * (i + 1)], in_=h_towers)
-        nc.vector.memset(h_rows[:, 4 * C : P], 1.0)
+        for i in range(2):
+            nc.sync.dma_start(out=h_rows[0:B, 2 * C * i : 2 * C * (i + 1)], in_=h_towers)
+        nc.vector.memset(h_rows[0:B, 4 * C : P], 1.0)
+        nc.vector.memset(h_rows[B:P, :], 1.0)
 
         tables = const.tile([P, RUNS // 2, P], BF16)
         for w, table in enumerate((W_emb, b_emb)):
@@ -101,6 +101,9 @@ def tile_mlp_embedding_layer_pa_kernel(tc, h_towers, W_emb, b_emb, M, out):
         make_identity(nc, ident_bf[:])
         ident_f32 = const.tile([P, P], F32)
         make_identity(nc, ident_f32[:])
+
+        twice = const.tile([P, B, 2], BF16)
+        nc.vector.tensor_copy(out=twice[:], in_=ident_bf[:, 0:B].unsqueeze(2).to_broadcast([P, B, 2]))
 
         pick = const.tile([P, 2 * C, TILE_B, 2], BF16)
         nc.vector.tensor_tensor(
@@ -246,15 +249,16 @@ def tile_mlp_embedding_layer_pa_kernel(tc, h_towers, W_emb, b_emb, M, out):
                         start=(g == 0),
                         stop=(g == PASSES - 1),
                     )
-            u_bf_of[(chunk, rt)] = u_out.tile([P, P, PACK], BF16, name="u_bf", align_bytes=64)
-            nc.scalar.copy(out=u_bf_of[(chunk, rt)][:], in_=u_bank[:].rearrange("p t r -> p r t"))
+            if rt % 2 == 0:
+                u_bf_of[(chunk, rt // 2)] = u_out.tile([P, 2, P, PACK], BF16, name="u_bf", align_bytes=64)
+            nc.scalar.copy(out=u_bf_of[(chunk, rt // 2)][:, rt % 2], in_=u_bank[:].rearrange("p t r -> p r t"))
 
-        def quantise_u(chunk, rt):
-            rows = slice(rt * P, (rt + 1) * P)
+        def quantise_u(chunk, pair):
+            rows = slice(pair * 2 * P, (pair + 1) * 2 * P)
             nc.vector.quantize_mx(
                 out=u_codes[:, chunk, rows].bitcast(FP8X4),
                 scales=u_scales[:, chunk, rows],
-                in_=u_bf_of[(chunk, rt)][:].rearrange("p r t -> p (r t)"),
+                in_=u_bf_of[(chunk, pair)][:].rearrange("p a r t -> p (a r t)"),
             )
 
         same_l = const.tile([P, TILE_B], F32)
@@ -304,7 +308,14 @@ def tile_mlp_embedding_layer_pa_kernel(tc, h_towers, W_emb, b_emb, M, out):
                 op=ALU.add,
             )
 
-        nc.tensor.transpose(out=h_own[:].rearrange("p b i -> p (b i)"), in_=h_rows[:], identity=ident_bf[:])
+        make_same_batch()
+        nc.tensor.matmul(
+            out=h_own[:].rearrange("p b i -> p (b i)"),
+            lhsT=h_rows[:],
+            rhs=twice[:].rearrange("p b i -> p (b i)"),
+            start=True,
+            stop=True,
+        )
         transpose_tables()
         for s in (LEFT, RIGHT):
             for pair in range(PAIRS):
@@ -321,7 +332,6 @@ def tile_mlp_embedding_layer_pa_kernel(tc, h_towers, W_emb, b_emb, M, out):
         for g in range(TENSOR_R_PASSES):
             for pair in range(PAIRS):
                 make_r_on_tensor(g, pair)
-        make_same_batch()
 
         for bank in range(BANKS + U_LAG):
             chunk, rt = bank // ROW_TILES, bank % ROW_TILES
@@ -348,8 +358,8 @@ def tile_mlp_embedding_layer_pa_kernel(tc, h_towers, W_emb, b_emb, M, out):
                         regroup_r(g)
                     if TENSOR_R_PASSES < g <= PASSES:
                         quantise_r(g - 1)
-            if bank >= U_LAG:
-                quantise_u((bank - U_LAG) // ROW_TILES, (bank - U_LAG) % ROW_TILES)
+            if bank >= U_LAG and (bank - U_LAG) % 2 == 1:
+                quantise_u((bank - U_LAG) // ROW_TILES, ((bank - U_LAG) % ROW_TILES) // 2)
         for rt in range(ROW_TILES):
             make_g(rt)
         for first_rt in range(0, ROW_TILES, TILES_IN_BANK):

@@ -29,8 +29,6 @@ BANKS = PASSES * ROW_TILES
 TILES_IN_BANK = 4
 LEFT, RIGHT = 0, 1
 TENSOR_R_PASSES = 2
-SCALAR_R_UNITS = (PASSES - TENSOR_R_PASSES) * C
-SCALAR_R_BANKS = (PASSES - 1) * ROW_TILES
 U_LAG = 3
 
 FLOPS = 2 * ROWS * E * E + 2 * B * C * C * E
@@ -76,14 +74,13 @@ def tile_mlp_embedding_layer_pa_kernel(tc, h_towers, W_emb, b_emb, M, out):
                 )
             return m_raw
 
-        m_raw_of = {0: load_m(0)}
+        m_raw_of = {0: load_m(0), 1: load_m(1)}
 
         h_all = const.tile([P, B, 2 * C], BF16)
         nc.sync.dma_start(
             out=h_all[:].rearrange("p b c -> p (b c)"),
             in_=h_towers.rearrange("b c -> (b c)").partition_broadcast(P),
         )
-        m_raw_of[1] = load_m(1)
 
         h_out = small.tile([2 * ROW_TILES, TILE_B, C], BF16)
         for s in (LEFT, RIGHT):
@@ -294,19 +291,23 @@ def tile_mlp_embedding_layer_pa_kernel(tc, h_towers, W_emb, b_emb, M, out):
                 out=tanh_of[rt][:],
                 in_=own[:],
                 func=ACT.Tanh,
+                scale=-1.0,
                 accum_out=sums[:, RIGHT * ROW_TILES + rt : RIGHT * ROW_TILES + rt + 1],
             )
 
-        def sum_over_i(first_rt):
-            turned = psum.tile([P, TILES_IN_BANK, P], F32, tag="bank")
-            for k in range(TILES_IN_BANK):
+        def sum_over_i(first_rt, tiles, on_scalar):
+            turned = psum.tile([P, tiles, P], F32, tag="bank")
+            for k in range(tiles):
                 nc.tensor.transpose(out=turned[:, k, :], in_=tanh_of[first_rt + k][:], identity=ident_f32[:])
-            nc.vector.tensor_reduce(
-                out=sums[:, LEFT * ROW_TILES + first_rt : LEFT * ROW_TILES + first_rt + TILES_IN_BANK],
-                in_=turned[:],
-                axis=AX.X,
-                op=ALU.add,
-            )
+            first = LEFT * ROW_TILES + first_rt
+            if on_scalar:
+                for k in range(tiles):
+                    unused = work.tile([P, P], F32, name="unused")
+                    nc.scalar.activation(
+                        out=unused[:], in_=turned[:, k, :], func=ACT.Identity, accum_out=sums[:, first + k : first + k + 1]
+                    )
+            else:
+                nc.vector.tensor_reduce(out=sums[:, first : first + tiles], in_=turned[:], axis=AX.X, op=ALU.add)
 
         make_same_batch()
         nc.tensor.matmul(
@@ -338,11 +339,11 @@ def tile_mlp_embedding_layer_pa_kernel(tc, h_towers, W_emb, b_emb, M, out):
             if bank < BANKS:
                 if rt == 0 and chunk + 2 < PASSES:
                     m_raw_of[chunk + 2] = load_m(chunk + 2)
-                if bank == 0:
+                if bank == ROW_TILES:
                     nc.scalar.copy(out=h_right[:], in_=h_all[:, :, C : 2 * C].rearrange("p b c -> p c b"))
-                for unit in range(SCALAR_R_UNITS):
-                    if unit * SCALAR_R_BANKS // SCALAR_R_UNITS == bank:
-                        make_r_on_scalar(TENSOR_R_PASSES + unit // C, unit % C)
+                if chunk in (1, 2):
+                    make_r_on_scalar(TENSOR_R_PASSES + chunk - 1, 2 * rt)
+                    make_r_on_scalar(TENSOR_R_PASSES + chunk - 1, 2 * rt + 1)
                 make_u(chunk, rt)
                 if chunk == 0 and rt < 2:
                     quantise_l(2 + rt)
@@ -362,33 +363,35 @@ def tile_mlp_embedding_layer_pa_kernel(tc, h_towers, W_emb, b_emb, M, out):
                 quantise_u((bank - U_LAG) // ROW_TILES, ((bank - U_LAG) % ROW_TILES) // 2)
         for rt in range(ROW_TILES):
             make_g(rt)
-        for first_rt in range(0, ROW_TILES, TILES_IN_BANK):
-            sum_over_i(first_rt)
+        sum_over_i(0, TILES_IN_BANK, True)
+        sum_over_i(TILES_IN_BANK, ROW_TILES - 1 - TILES_IN_BANK, False)
+        sum_over_i(ROW_TILES - 1, 1, False)
 
         Q = 2 * ROW_TILES
         sums_t = psum.tile([P, P], F32, tag="bank")
         nc.tensor.transpose(out=sums_t[:], in_=sums[:], identity=ident_f32[:])
-        by_batch = sums_t[0:Q, :].rearrange("q (c l) -> q l c", l=TILE_B)
-        top = small.tile([Q, TILE_B], F32)
-        nc.vector.tensor_reduce(out=top[:], in_=by_batch, axis=AX.X, op=ALU.max)
-        shifted = small.tile([Q, TILE_B, C], F32)
-        nc.vector.tensor_tensor(
-            out=shifted[:], in0=by_batch, in1=top[:].unsqueeze(2).to_broadcast([Q, TILE_B, C]), op=ALU.subtract
-        )
+        lowest = small.tile([Q, 1], F32)
+        nc.vector.tensor_reduce(out=lowest[:], in_=sums_t[0:Q, :], axis=AX.X, op=ALU.min)
         grown = small.tile([Q, TILE_B, C], F32)
-        nc.scalar.activation(out=grown[:], in_=shifted[:], func=ACT.Exp)
+        nc.scalar.activation(
+            out=grown[:],
+            in_=sums_t[0:Q, :].rearrange("q (c l) -> q l c", l=TILE_B),
+            func=ACT.Exp,
+            scale=-1.0,
+            bias=lowest[:, 0:1],
+        )
         total = small.tile([Q, TILE_B], F32)
         nc.vector.tensor_reduce(out=total[:], in_=grown[:], axis=AX.X, op=ALU.add)
-        share = small.tile([Q, TILE_B], F32)
-        nc.vector.reciprocal(out=share[:], in_=total[:])
         gated = small.tile([Q, TILE_B, C], F32)
         nc.vector.tensor_tensor(out=gated[:], in0=grown[:], in1=h_out[:], op=ALU.mult)
+        share = small.tile([Q, TILE_B], F32)
+        nc.vector.reciprocal(out=share[:], in_=total[:])
         result = small.tile([Q, TILE_B, C], F32)
         nc.vector.tensor_tensor(
             out=result[:], in0=gated[:], in1=share[:].unsqueeze(2).to_broadcast([Q, TILE_B, C]), op=ALU.mult
         )
-        for s in (LEFT, RIGHT):
-            nc.sync.dma_start(
+        for s, queue in ((LEFT, nc.sync), (RIGHT, nc.scalar)):
+            queue.dma_start(
                 out=out[:, s * C : (s + 1) * C].rearrange("(r l) c -> r l c", l=TILE_B),
                 in_=result[s * ROW_TILES : (s + 1) * ROW_TILES, :, :],
             )

@@ -29,6 +29,8 @@ BANKS = PASSES * ROW_TILES
 TILES_IN_BANK = 4
 LEFT, RIGHT = 0, 1
 TENSOR_R_PASSES = 2
+SCALAR_D_0 = 2 * TENSOR_R_PASSES
+WARM_UPS = 3
 U_LAG = 3
 
 FLOPS = 2 * ROWS * E * E + 2 * B * C * C * E
@@ -48,6 +50,12 @@ def tile_mlp_embedding_layer_pa_kernel(tc, h_towers, W_emb, b_emb, M, out):
         small = ctx.enter_context(tc.tile_pool(name="small", bufs=1))
         psum = ctx.enter_context(tc.psum_pool(name="psum", bufs=8))
         ctx.enter_context(tc.manual_schedule())
+
+        zeros = const.tile([P, K_PASS], BF16)
+        nc.vector.memset(zeros[:], 0.0)
+        idle_bank = psum.tile([P, K_PASS], F32, tag="bank")
+        for k in range(WARM_UPS):
+            nc.tensor.matmul(out=idle_bank[:], lhsT=zeros[:, 0:P], rhs=zeros[:], start=True, stop=True)
 
         h_rows = const.tile([P, P], BF16)
         for i in range(2):
@@ -179,13 +187,13 @@ def tile_mlp_embedding_layer_pa_kernel(tc, h_towers, W_emb, b_emb, M, out):
                 in_=r_bf_of[g][:].rearrange("p a w -> p (a w)"),
             )
 
-        tables_t = const.tile([P, RUNS // 2, P], F32)
+        tables_t = const.tile([P, RUNS // 2 - SCALAR_D_0, P], F32)
         h_right = const.tile([P, C, B], BF16)
 
         def transpose_tables():
-            t_bank = psum.tile([P, RUNS // 2, P], BF16, tag="bank")
-            for d in range(RUNS // 2):
-                nc.tensor.transpose(out=t_bank[:, d, :], in_=tables[:, d, :], identity=ident_bf[:])
+            t_bank = psum.tile([P, RUNS // 2 - SCALAR_D_0, P], BF16, tag="bank")
+            for d in range(SCALAR_D_0, RUNS // 2):
+                nc.tensor.transpose(out=t_bank[:, d - SCALAR_D_0, :], in_=tables[:, d, :], identity=ident_bf[:])
             nc.scalar.copy(out=tables_t[:], in_=t_bank[:])
 
         r_parts_of = {}
@@ -201,8 +209,8 @@ def tile_mlp_embedding_layer_pa_kernel(tc, h_towers, W_emb, b_emb, M, out):
                     out=r_parts_of[g][:, :, j, t, :],
                     in_=h_right[:, j, :].rearrange("p (r l) -> p r l", l=TILE_B),
                     func=ACT.Identity,
-                    scale=tables_t[:, 2 * g + t // 2, column : column + 1],
-                    bias=tables_t[:, 2 * g + t // 2, 64 + column : 64 + column + 1],
+                    scale=tables_t[:, 2 * g + t // 2 - SCALAR_D_0, column : column + 1],
+                    bias=tables_t[:, 2 * g + t // 2 - SCALAR_D_0, 64 + column : 64 + column + 1],
                 )
 
         def regroup_r(g):

@@ -30,6 +30,7 @@ TILES_IN_BANK = 4
 LEFT, RIGHT = 0, 1
 TENSOR_R_PASSES = 2
 SCALAR_D_0 = 2 * TENSOR_R_PASSES
+WIDE_BANKS = tuple(range(ROW_TILES)) + tuple(range(BANKS - ROW_TILES, BANKS - 2))
 WARM_UPS = 3
 U_LAG = 3
 
@@ -258,6 +259,28 @@ def tile_mlp_embedding_layer_pa_kernel(tc, h_towers, W_emb, b_emb, M, out):
                 u_bf_of[(chunk, rt // 2)] = u_out.tile([P, 2, P, PACK], BF16, name="u_bf", align_bytes=64)
             nc.scalar.copy(out=u_bf_of[(chunk, rt // 2)][:, rt % 2], in_=u_bank[:].rearrange("p t r -> p r t"))
 
+        def make_u_wide(chunk, pair, half):
+            u_bank = psum.tile([P, 2, 2 * P], F32, tag="bank")
+            for i in range(2):
+                t = 2 * half + i
+                n_cols = slice((chunk * PACK + t) * P, (chunk * PACK + t + 1) * P)
+                for g in range(PASSES):
+                    nc.tensor.matmul_mx(
+                        out=u_bank[:, i, :],
+                        lhsT=m_codes[:, g, n_cols].bitcast(FP8X4),
+                        lhsT_scale=m_scales[:, g, n_cols],
+                        rhs=l_codes[:, pair, g, :].bitcast(FP8X4),
+                        rhs_scale=l_scales[:, pair, g, :],
+                        start=(g == 0),
+                        stop=(g == PASSES - 1),
+                    )
+            if half == 0:
+                u_bf_of[(chunk, pair)] = u_out.tile([P, 2, P, PACK], BF16, name="u_bf", align_bytes=64)
+            nc.scalar.copy(
+                out=u_bf_of[(chunk, pair)][:].rearrange("p a r t -> p (a r) t")[:, :, 2 * half : 2 * half + 2],
+                in_=u_bank[:].rearrange("p i r -> p r i"),
+            )
+
         def quantise_u(chunk, pair):
             rows = slice(pair * 2 * P, (pair + 1) * 2 * P)
             nc.vector.quantize_mx(
@@ -352,7 +375,10 @@ def tile_mlp_embedding_layer_pa_kernel(tc, h_towers, W_emb, b_emb, M, out):
                 if chunk in (1, 2):
                     make_r_on_scalar(TENSOR_R_PASSES + chunk - 1, 2 * rt)
                     make_r_on_scalar(TENSOR_R_PASSES + chunk - 1, 2 * rt + 1)
-                make_u(chunk, rt)
+                if bank in WIDE_BANKS:
+                    make_u_wide(chunk, rt // 2, rt % 2)
+                else:
+                    make_u(chunk, rt)
                 if chunk == 0 and rt < 2:
                     quantise_l(2 + rt)
                 if chunk + 1 < PASSES and rt < PASSES:

from contextlib import ExitStack

import concourse.mybir as mybir
from concourse.masks import make_identity

F32 = mybir.dt.float32
BF16 = mybir.dt.bfloat16
U32 = mybir.dt.uint32
U8 = mybir.dt.uint8
FP8X4 = mybir.dt.float8_e4m3fn_x4
ACT = mybir.ActivationFunctionType
ALU = mybir.AluOpType
AX = mybir.AxisListType

P = 128
PACK = 4
K_PASS = P * PACK
B = 64
C = 16
E = 2048
PASSES = E // K_PASS
RUNS = E // P
TILE_B = P // C
ROW_TILES = B // TILE_B
PAIRS = ROW_TILES // 2
ROWS = B * C
CHUNK = K_PASS
BANKS = PASSES * ROW_TILES
TILES_IN_BANK = 4
LEFT, RIGHT = 0, 1
TENSOR_R_PASSES = 2
SCALAR_D_0 = 2 * TENSOR_R_PASSES
WIDE_BANKS = tuple(range(ROW_TILES)) + tuple(range(BANKS - ROW_TILES, BANKS - 2))
WARM_UPS = 3
U_LAG = 3

FLOPS = 2 * ROWS * E * E + 2 * B * C * C * E


def tile_mlp_embedding_layer_pa_kernel(tc, h_towers, W_emb, b_emb, M, out):
    nc = tc.nc
    with ExitStack() as ctx:
        const = ctx.enter_context(tc.tile_pool(name="const", bufs=1))
        keep = ctx.enter_context(tc.tile_pool(name="keep", bufs=1))
        m_in = ctx.enter_context(tc.tile_pool(name="m_in", bufs=2))
        m_words = ctx.enter_context(tc.tile_pool(name="m_words", bufs=3))
        wide = ctx.enter_context(tc.tile_pool(name="wide", bufs=5))
        work = ctx.enter_context(tc.tile_pool(name="work", bufs=4))
        u_out = ctx.enter_context(tc.tile_pool(name="u_out", bufs=8))
        tanh_pool = ctx.enter_context(tc.tile_pool(name="tanh_pool", bufs=8))
        small = ctx.enter_context(tc.tile_pool(name="small", bufs=1))
        psum = ctx.enter_context(tc.psum_pool(name="psum", bufs=8))
        ctx.enter_context(tc.manual_schedule())

        zeros = const.tile([P, K_PASS], BF16)
        nc.vector.memset(zeros[:], 0.0)
        idle_bank = psum.tile([P, K_PASS], F32, tag="bank")
        for k in range(WARM_UPS):
            nc.tensor.matmul(out=idle_bank[:], lhsT=zeros[:, 0:P], rhs=zeros[:], start=True, stop=True)

        h_rows = const.tile([P, P], BF16)
        for i in range(2):
            nc.sync.dma_start(out=h_rows[0:B, 2 * C * i : 2 * C * (i + 1)], in_=h_towers)
        nc.vector.memset(h_rows[0:B, 4 * C : P], 1.0)
        nc.vector.memset(h_rows[B:P, :], 1.0)

        tables = const.tile([P, RUNS // 2, P], BF16)
        for w, table in enumerate((W_emb, b_emb)):
            for i in range(2):
                first = 64 * w + 2 * C * i
                nc.sync.dma_start(
                    out=tables[first : first + 2 * C, :, :],
                    in_=table.rearrange("c (d i p) -> i c d p", i=2, p=P)[i],
                )

        def load_m(chunk):
            m_raw = m_in.tile([P, RUNS, CHUNK], BF16)
            for g in range(PASSES):
                runs = slice(g * PACK, (g + 1) * PACK)
                nc.sync.dma_start(
                    out=m_raw[:, runs, :],
                    in_=M.rearrange("(run p) n -> p run n", p=P)[:, runs, chunk * CHUNK : (chunk + 1) * CHUNK],
                )
            return m_raw

        m_raw_of = {0: load_m(0), 1: load_m(1)}

        h_all = const.tile([P, B, 2 * C], BF16)
        nc.sync.dma_start(
            out=h_all[:].rearrange("p b c -> p (b c)"),
            in_=h_towers.rearrange("b c -> (b c)").partition_broadcast(P),
        )

        h_out = small.tile([2 * ROW_TILES, TILE_B, C], BF16)
        for s in (LEFT, RIGHT):
            nc.sync.dma_start(
                out=h_out[s * ROW_TILES : (s + 1) * ROW_TILES, :, :],
                in_=h_towers[:, s * C : (s + 1) * C].rearrange("(r l) c -> r l c", l=TILE_B),
            )

        first_in = small.tile([P, 1], F32)
        nc.vector.memset(first_in[:], 0.0)
        first_out = small.tile([P, 1], F32)
        nc.scalar.activation(out=first_out[:], in_=first_in[:], func=ACT.Tanh)

        ident_bf = const.tile([P, P], BF16)
        make_identity(nc, ident_bf[:])
        ident_f32 = const.tile([P, P], F32)
        make_identity(nc, ident_f32[:])

        twice = const.tile([P, B, 2], BF16)
        nc.vector.tensor_copy(out=twice[:], in_=ident_bf[:, 0:B].unsqueeze(2).to_broadcast([P, B, 2]))

        pick = const.tile([P, 2 * C, TILE_B, 2], BF16)
        nc.vector.tensor_tensor(
            out=pick[:],
            in0=ident_bf[:, 0:64].rearrange("p (i c) -> p c i", i=2).unsqueeze(2).to_broadcast([P, 2 * C, TILE_B, 2]),
            in1=ident_bf[:, 64:128].rearrange("p (i c) -> p c i", i=2).unsqueeze(2).to_broadcast([P, 2 * C, TILE_B, 2]),
            op=ALU.add,
        )

        sums = small.tile([P, P], F32)
        nc.gpsimd.memset(sums[:], 0.0)

        m_codes = keep.tile([P, PASSES, E], U32, align_bytes=64)
        m_scales = keep.tile([P, PASSES, E], U8, align_bytes=64)
        l_codes = keep.tile([P, PAIRS, PASSES, 2 * P], U32, align_bytes=64)
        l_scales = keep.tile([P, PAIRS, PASSES, 2 * P], U8, align_bytes=64)
        u_codes = keep.tile([P, PASSES, ROWS], U32, align_bytes=64)
        u_scales = keep.tile([P, PASSES, ROWS], U8, align_bytes=64)
        r_codes = keep.tile([P, PASSES, ROWS], U32, align_bytes=64)
        r_scales = keep.tile([P, PASSES, ROWS], U8, align_bytes=64)

        h_own = psum.tile([P, B, 2], BF16, tag="bank")
        spread_of = {}
        for s in (LEFT, RIGHT):
            spread_of[s] = const.tile([P, ROW_TILES, C, TILE_B, 2], BF16, name="spread%d" % s)

        def spread_h(s, pair):
            shape = [P, 2, C, 2 * TILE_B]
            nc.vector.tensor_tensor(
                out=spread_of[s][:, 2 * pair : 2 * pair + 2].rearrange("p r c l i -> p r c (l i)"),
                in0=h_own[:, 2 * pair * TILE_B : 2 * (pair + 1) * TILE_B, :]
                .rearrange("p (r l) i -> p r (l i)", r=2)
                .unsqueeze(2)
                .to_broadcast(shape),
                in1=pick[:, s * C : (s + 1) * C].rearrange("p c l i -> p c (l i)").unsqueeze(1).to_broadcast(shape),
                op=ALU.mult,
            )

        def make_emb(s, pair, g, emb_bf):
            e_bank = psum.tile([P, 2 * P, 2, 2], BF16, tag="bank")
            for half in range(2):
                nc.tensor.matmul(
                    out=e_bank[:, :, half, :],
                    lhsT=tables[:, 2 * g + half, :],
                    rhs=spread_of[s][:, 2 * pair : 2 * pair + 2].rearrange("p r c l i -> p (r c l) i"),
                    start=True,
                    stop=True,
                )
            nc.scalar.copy(out=emb_bf, in_=e_bank[:].rearrange("p r h i -> p (r h i)"))

        l_bf_of = {}

        def make_l(pair, g):
            if g == 0:
                l_bf_of[pair] = wide.tile([P, PASSES, 2 * K_PASS], BF16, tag="wide", name="l_bf", align_bytes=64)
            make_emb(LEFT, pair, g, l_bf_of[pair][:, g, :])

        def quantise_l(pair):
            nc.vector.quantize_mx(
                out=l_codes[:, pair].rearrange("p g w -> p (g w)").bitcast(FP8X4),
                scales=l_scales[:, pair].rearrange("p g w -> p (g w)"),
                in_=l_bf_of[pair][:].rearrange("p g w -> p (g w)"),
            )

        r_bf_of = {}

        def make_r_on_tensor(g, pair):
            if pair == 0:
                r_bf_of[g] = wide.tile([P, PAIRS, 2 * K_PASS], BF16, tag="wide", name="r_bf", align_bytes=64)
            make_emb(RIGHT, pair, g, r_bf_of[g][:, pair, :])

        def quantise_r(g):
            nc.vector.quantize_mx(
                out=r_codes[:, g, :].bitcast(FP8X4),
                scales=r_scales[:, g, :],
                in_=r_bf_of[g][:].rearrange("p a w -> p (a w)"),
            )

        tables_t = const.tile([P, RUNS // 2 - SCALAR_D_0, P], F32)
        h_right = const.tile([P, C, B], BF16)

        def transpose_tables():
            t_bank = psum.tile([P, RUNS // 2 - SCALAR_D_0, P], BF16, tag="bank")
            for d in range(SCALAR_D_0, RUNS // 2):
                nc.tensor.transpose(out=t_bank[:, d - SCALAR_D_0, :], in_=tables[:, d, :], identity=ident_bf[:])
            nc.scalar.copy(out=tables_t[:], in_=t_bank[:])

        r_parts_of = {}

        def make_r_on_scalar(g, j):
            if j == 0:
                r_parts_of[g] = wide.tile(
                    [P, ROW_TILES, C, PACK, TILE_B], BF16, tag="wide", name="r_parts", align_bytes=64
                )
            for t in range(PACK):
                column = 2 * C * (t % 2) + C + j
                nc.scalar.activation(
                    out=r_parts_of[g][:, :, j, t, :],
                    in_=h_right[:, j, :].rearrange("p (r l) -> p r l", l=TILE_B),
                    func=ACT.Identity,
                    scale=tables_t[:, 2 * g + t // 2 - SCALAR_D_0, column : column + 1],
                    bias=tables_t[:, 2 * g + t // 2 - SCALAR_D_0, 64 + column : 64 + column + 1],
                )

        def regroup_r(g):
            r_bf_of[g] = wide.tile([P, PAIRS, 2 * K_PASS], BF16, tag="wide", name="r_bf", align_bytes=64)
            nc.vector.tensor_copy(
                out=r_bf_of[g][:].rearrange("p a (b l t) -> p (a b) l t", l=TILE_B, t=PACK),
                in_=r_parts_of[g][:].rearrange("p r j t l -> p (r j) l t"),
            )

        m_bf_of = {}

        def regroup_m(chunk, g):
            m_bf_of[g] = m_words.tile([P, CHUNK, PACK], BF16, name="m_bf", align_bytes=64)
            nc.vector.tensor_copy(
                out=m_bf_of[g][:].rearrange("p (c x) t -> p c t x", x=4),
                in_=m_raw_of[chunk][:, g * PACK : (g + 1) * PACK, :].rearrange("p t (c x) -> p c t x", x=4),
            )

        def quantise_m(chunk, g):
            cols = slice(chunk * CHUNK, (chunk + 1) * CHUNK)
            nc.vector.quantize_mx(
                out=m_codes[:, g, cols].bitcast(FP8X4),
                scales=m_scales[:, g, cols],
                in_=m_bf_of[g][:].rearrange("p n t -> p (n t)"),
            )

        u_bf_of = {}

        def make_u(chunk, rt):
            l_rows = slice((rt % 2) * P, (rt % 2 + 1) * P)
            u_bank = psum.tile([P, PACK, P], F32, tag="bank")
            for t in range(PACK):
                n_cols = slice((chunk * PACK + t) * P, (chunk * PACK + t + 1) * P)
                for g in range(PASSES):
                    nc.tensor.matmul_mx(
                        out=u_bank[:, t, :],
                        lhsT=m_codes[:, g, n_cols].bitcast(FP8X4),
                        lhsT_scale=m_scales[:, g, n_cols],
                        rhs=l_codes[:, rt // 2, g, l_rows].bitcast(FP8X4),
                        rhs_scale=l_scales[:, rt // 2, g, l_rows],
                        start=(g == 0),
                        stop=(g == PASSES - 1),
                    )
            if rt % 2 == 0:
                u_bf_of[(chunk, rt // 2)] = u_out.tile([P, 2, P, PACK], BF16, name="u_bf", align_bytes=64)
            nc.scalar.copy(out=u_bf_of[(chunk, rt // 2)][:, rt % 2], in_=u_bank[:].rearrange("p t r -> p r t"))

        def make_u_wide(chunk, pair, half):
            u_bank = psum.tile([P, 2, 2 * P], F32, tag="bank")
            for i in range(2):
                t = 2 * half + i
                n_cols = slice((chunk * PACK + t) * P, (chunk * PACK + t + 1) * P)
                for g in range(PASSES):
                    nc.tensor.matmul_mx(
                        out=u_bank[:, i, :],
                        lhsT=m_codes[:, g, n_cols].bitcast(FP8X4),
                        lhsT_scale=m_scales[:, g, n_cols],
                        rhs=l_codes[:, pair, g, :].bitcast(FP8X4),
                        rhs_scale=l_scales[:, pair, g, :],
                        start=(g == 0),
                        stop=(g == PASSES - 1),
                    )
            if half == 0:
                u_bf_of[(chunk, pair)] = u_out.tile([P, 2, P, PACK], BF16, name="u_bf", align_bytes=64)
            nc.scalar.copy(
                out=u_bf_of[(chunk, pair)][:].rearrange("p a r t -> p (a r) t")[:, :, 2 * half : 2 * half + 2],
                in_=u_bank[:].rearrange("p i r -> p r i"),
            )

        def quantise_u(chunk, pair):
            rows = slice(pair * 2 * P, (pair + 1) * 2 * P)
            nc.vector.quantize_mx(
                out=u_codes[:, chunk, rows].bitcast(FP8X4),
                scales=u_scales[:, chunk, rows],
                in_=u_bf_of[(chunk, pair)][:].rearrange("p a r t -> p (a r t)"),
            )

        same_l = const.tile([P, TILE_B], F32)
        same_batch = const.tile([P, C, TILE_B], F32)

        def make_same_batch():
            nc.vector.tensor_reduce(
                out=same_l[:], in_=ident_f32[:].rearrange("p (c l) -> p l c", l=TILE_B), axis=AX.X, op=ALU.add
            )
            nc.vector.tensor_copy(out=same_batch[:], in_=same_l[:].unsqueeze(1).to_broadcast([P, C, TILE_B]))

        tanh_of = {}

        def make_g(rt):
            rows = slice(rt * P, (rt + 1) * P)
            g_bank = psum.tile([P, P], F32, tag="bank")
            for g in range(PASSES):
                nc.tensor.matmul_mx(
                    out=g_bank[:],
                    lhsT=u_codes[:, g, rows].bitcast(FP8X4),
                    lhsT_scale=u_scales[:, g, rows],
                    rhs=r_codes[:, g, rows].bitcast(FP8X4),
                    rhs_scale=r_scales[:, g, rows],
                    start=(g == 0),
                    stop=(g == PASSES - 1),
                )
            own = work.tile([P, P], F32)
            nc.vector.tensor_tensor(
                out=own[:], in0=g_bank[:], in1=same_batch[:].rearrange("p c l -> p (c l)"), op=ALU.mult
            )
            tanh_of[rt] = tanh_pool.tile([P, P], F32, name="tanh_g")
            nc.scalar.activation(
                out=tanh_of[rt][:],
                in_=own[:],
                func=ACT.Tanh,
                scale=-1.0,
                accum_out=sums[:, RIGHT * ROW_TILES + rt : RIGHT * ROW_TILES + rt + 1],
            )

        def sum_over_i(first_rt, tiles, on_scalar):
            turned = psum.tile([P, tiles, P], F32, tag="bank")
            for k in range(tiles):
                nc.tensor.transpose(out=turned[:, k, :], in_=tanh_of[first_rt + k][:], identity=ident_f32[:])
            first = LEFT * ROW_TILES + first_rt
            if on_scalar:
                for k in range(tiles):
                    unused = work.tile([P, P], F32, name="unused")
                    nc.scalar.activation(
                        out=unused[:], in_=turned[:, k, :], func=ACT.Identity, accum_out=sums[:, first + k : first + k + 1]
                    )
            else:
                nc.vector.tensor_reduce(out=sums[:, first : first + tiles], in_=turned[:], axis=AX.X, op=ALU.add)

        make_same_batch()
        nc.tensor.matmul(
            out=h_own[:].rearrange("p b i -> p (b i)"),
            lhsT=h_rows[:],
            rhs=twice[:].rearrange("p b i -> p (b i)"),
            start=True,
            stop=True,
        )
        transpose_tables()
        for s in (LEFT, RIGHT):
            for pair in range(PAIRS):
                spread_h(s, pair)
        for pair in range(PAIRS):
            regroup_m(0, pair)
            if pair > 0:
                quantise_m(0, pair - 1)
            for g in range(PASSES):
                make_l(pair, g)
        quantise_m(0, PASSES - 1)
        quantise_l(0)
        quantise_l(1)
        for g in range(TENSOR_R_PASSES):
            for pair in range(PAIRS):
                make_r_on_tensor(g, pair)

        for bank in range(BANKS + U_LAG):
            chunk, rt = bank // ROW_TILES, bank % ROW_TILES
            if bank < BANKS:
                if rt == 0 and chunk + 2 < PASSES:
                    m_raw_of[chunk + 2] = load_m(chunk + 2)
                if bank == ROW_TILES:
                    nc.scalar.copy(out=h_right[:], in_=h_all[:, :, C : 2 * C].rearrange("p b c -> p c b"))
                if chunk in (1, 2):
                    make_r_on_scalar(TENSOR_R_PASSES + chunk - 1, 2 * rt)
                    make_r_on_scalar(TENSOR_R_PASSES + chunk - 1, 2 * rt + 1)
                if bank in WIDE_BANKS:
                    make_u_wide(chunk, rt // 2, rt % 2)
                else:
                    make_u(chunk, rt)
                if chunk == 0 and rt < 2:
                    quantise_l(2 + rt)
                if chunk + 1 < PASSES and rt < PASSES:
                    regroup_m(chunk + 1, rt)
                if chunk + 1 < PASSES and 0 < rt <= PASSES:
                    quantise_m(chunk + 1, rt - 1)
                if chunk == 1 and rt >= ROW_TILES - TENSOR_R_PASSES:
                    quantise_r(rt - (ROW_TILES - TENSOR_R_PASSES))
                if chunk == PASSES - 1 and rt % 2 == 0:
                    g = TENSOR_R_PASSES + rt // 2
                    if g < PASSES:
                        regroup_r(g)
                    if TENSOR_R_PASSES < g <= PASSES:
                        quantise_r(g - 1)
            if bank >= U_LAG and (bank - U_LAG) % 2 == 1:
                quantise_u((bank - U_LAG) // ROW_TILES, ((bank - U_LAG) % ROW_TILES) // 2)
        for rt in range(ROW_TILES):
            make_g(rt)
        sum_over_i(0, TILES_IN_BANK, True)
        sum_over_i(TILES_IN_BANK, ROW_TILES - 1 - TILES_IN_BANK, False)
        sum_over_i(ROW_TILES - 1, 1, False)

        Q = 2 * ROW_TILES
        sums_t = psum.tile([P, P], F32, tag="bank")
        nc.tensor.transpose(out=sums_t[:], in_=sums[:], identity=ident_f32[:])
        lowest = small.tile([Q, 1], F32)
        nc.vector.tensor_reduce(out=lowest[:], in_=sums_t[0:Q, :], axis=AX.X, op=ALU.min)
        grown = small.tile([Q, TILE_B, C], F32)
        nc.scalar.activation(
            out=grown[:],
            in_=sums_t[0:Q, :].rearrange("q (c l) -> q l c", l=TILE_B),
            func=ACT.Exp,
            scale=-1.0,
            bias=lowest[:, 0:1],
        )
        total = small.tile([Q, TILE_B], F32)
        nc.vector.tensor_reduce(out=total[:], in_=grown[:], axis=AX.X, op=ALU.add)
        gated = small.tile([Q, TILE_B, C], F32)
        nc.vector.tensor_tensor(out=gated[:], in0=grown[:], in1=h_out[:], op=ALU.mult)
        share = small.tile([Q, TILE_B], F32)
        nc.vector.reciprocal(out=share[:], in_=total[:])
        result = small.tile([Q, TILE_B, C], F32)
        nc.vector.tensor_tensor(
            out=result[:], in0=gated[:], in1=share[:].unsqueeze(2).to_broadcast([Q, TILE_B, C]), op=ALU.mult
        )
        for s, queue in ((LEFT, nc.sync), (RIGHT, nc.scalar)):
            queue.dma_start(
                out=out[:, s * C : (s + 1) * C].rearrange("(r l) c -> r l c", l=TILE_B),
                in_=result[s * ROW_TILES : (s + 1) * ROW_TILES, :, :],
            )
